import numpy as np
import ml_dtypes


def mxq(x, axis, fmt="e4m3"):
    dtype, down = {"e4m3": (ml_dtypes.float8_e4m3fn, 7), "e5m2": (ml_dtypes.float8_e5m2, 14)}[fmt]
    v = np.moveaxis(np.asarray(x, np.float32).astype(ml_dtypes.bfloat16).astype(np.float64), axis, -1)
    blocks = v.reshape(v.shape[:-1] + (-1, 32))
    amax = np.abs(blocks).max(-1, keepdims=True)
    byte = np.maximum(np.where(amax > 0, np.frexp(amax)[1] - 1 + 127, 0) - down, 1)
    scale = np.exp2(byte - 127.0)
    codes = (blocks / scale).astype(np.float32).astype(dtype).astype(np.float64)
    return np.moveaxis((codes * scale).reshape(v.shape), -1, axis)


WIDE = False


def mx_kscale(k):
    if not WIDE:
        return np.ones(k)
    levels = np.array([10, -10, 5, -5, 0])
    a = np.random.permutation(np.resize(levels, k // 512 * 4)).reshape(k // 512, 4)
    idx = np.arange(k)
    return np.exp2(a[idx // 512, idx % 128 // 32])


BF16 = ml_dtypes.bfloat16


def bf(x):
    return np.asarray(x, np.float32).astype(BF16)


def f64(x):
    return np.asarray(x).astype(np.float64)


B, C, IC, H, W = 2, 1024, 512, 32, 32
N = H * W


def setup_inputs():
    t = mx_kscale(IC)
    a = 1.2 * IC ** -0.25
    return {"theta": bf(np.random.standard_normal((B, IC, N)) * a),
            "phi": bf(np.random.standard_normal((B, IC, N)) * a),
            "g_proj": bf(np.random.standard_normal((B, IC, N)) * t[None, :, None]),
            "pos_embedding": bf(np.random.standard_normal((1, N, N))),
            "pos_embedding_decoder": bf((1.5 + 0.5 * np.random.standard_normal((1, IC, H, W))) * t[None, :, None, None]),
            "w_mask": bf(np.random.standard_normal((C, IC)) * 2.0 / np.sqrt(IC) / t[None, :]),
            "x": bf(np.random.standard_normal((B, C, H, W)))}


def reference(theta, phi, g_proj, pos_embedding, pos_embedding_decoder, w_mask, x):
    s = f64(theta).transpose(0, 2, 1) @ f64(phi) + f64(pos_embedding)
    e = np.exp(s - s.max(1, keepdims=True))
    attn = e / e.sum(1, keepdims=True)
    g = (f64(g_proj) + f64(pos_embedding_decoder).reshape(1, IC, N)).transpose(0, 2, 1)
    y = mxq(attn, 2, "e4m3") @ mxq(g, 1, "e4m3")
    m = mxq(f64(w_mask), 1, "e4m3") @ mxq(y.transpose(0, 2, 1), 1, "e4m3")
    return m.reshape(B, C, H, W) + f64(x)

@@ -1,0 +1,284 @@
+from contextlib import ExitStack
+
+import concourse.mybir as mybir
+from concourse.masks import make_identity
+
+F32 = mybir.dt.float32
+BF16 = mybir.dt.bfloat16
+U32 = mybir.dt.uint32
+U8 = mybir.dt.uint8
+FP8X4 = mybir.dt.float8_e4m3fn_x4
+ADD = mybir.AluOpType.add
+MAX = mybir.AluOpType.max
+EXP = mybir.ActivationFunctionType.Exp
+COPY = mybir.ActivationFunctionType.Copy
+X_AXIS = mybir.AxisListType.X
+
+B = 2
+IC = 512
+C = 1024
+N = 1024
+P = 128
+PACK = 4
+BANK = 512
+K_PASS = P * PACK
+J_PASSES = N // K_PASS
+J_BLOCKS = N // P
+I_HALVES = N // BANK
+IC_CHUNKS = IC // P
+O_BLOCKS = C // P
+
+FLOPS = 3 * 2 * B * N * N * IC
+
+
+def tile_nonlocalblock_pa_kernel(
+    tc, theta, phi, g_proj, pos_embedding, pos_embedding_decoder, w_mask, x, out
+):
+    nc = tc.nc
+    x_rows = x.rearrange("b o h w -> b o (h w)")
+    out_rows = out.rearrange("b o h w -> b o (h w)")
+
+    with ExitStack() as stack:
+        const = stack.enter_context(tc.tile_pool(name="const", bufs=1))
+        inputs = stack.enter_context(tc.tile_pool(name="inputs", bufs=2))
+        g_pool = stack.enter_context(tc.tile_pool(name="g_pool", bufs=1))
+        soft = stack.enter_context(tc.tile_pool(name="soft", bufs=2))
+        stats = stack.enter_context(tc.tile_pool(name="stats", bufs=8))
+        codes = stack.enter_context(tc.tile_pool(name="codes", bufs=2))
+        psum_s = stack.enter_context(tc.psum_pool(name="psum_s", bufs=3))
+        psum_t = stack.enter_context(tc.psum_pool(name="psum_t", bufs=3))
+        psum_m = stack.enter_context(tc.psum_pool(name="psum_m", bufs=2))
+
+        ident_bf = const.tile([P, P], BF16, name="ident_bf")
+        make_identity(nc, ident_bf[:])
+        ident_f32 = const.tile([P, P], F32, name="ident_f32")
+        make_identity(nc, ident_f32[:])
+
+        theta_sb = []
+        phi_sb = []
+        for b in range(B):
+            theta_sb.append(inputs.tile([P, IC_CHUNKS, N], BF16, name="theta_sb", tag="theta"))
+            phi_sb.append(inputs.tile([P, IC_CHUNKS, N], BF16, name="phi_sb", tag="phi"))
+
+        def load_theta(b):
+            nc.sync.dma_start(out=theta_sb[b][:], in_=theta[b].rearrange("(k p) i -> p k i", p=P))
+
+        def load_phi(b, g):
+            cols = slice(g * K_PASS, (g + 1) * K_PASS)
+            nc.sync.dma_start(
+                out=phi_sb[b][:, :, cols], in_=phi[b, :, cols].rearrange("(k p) j -> p k j", p=P)
+            )
+
+        pos_t = const.tile([P, J_BLOCKS, N], BF16, name="pos_t")
+        w_codes = const.tile([P, C], U32, name="w_codes", align_bytes=64)
+        w_scales = const.tile([P, C], U8, name="w_scales", align_bytes=64)
+        ped_sb = const.tile([P, PACK, N], BF16, name="ped_sb")
+
+        with tc.tile_pool(name="head", bufs=1) as head:
+            pos_sb = []
+            for g in range(J_PASSES):
+                pos_sb.append(head.tile([P, J_BLOCKS, K_PASS], BF16, name="pos_sb%d" % g))
+
+            def load_pos(g):
+                cols = slice(g * K_PASS, (g + 1) * K_PASS)
+                nc.sync.dma_start(
+                    out=pos_sb[g][:], in_=pos_embedding[0, :, cols].rearrange("(a p) j -> p a j", p=P)
+                )
+
+            load_pos(0)
+            load_theta(0)
+            load_phi(0, 0)
+            load_pos(1)
+            load_phi(0, 1)
+            w_sb = head.tile([P, O_BLOCKS, IC], BF16, name="w_sb")
+            nc.sync.dma_start(out=w_sb[:], in_=w_mask.rearrange("(a p) c -> p a c", p=P))
+
+            for g in range(J_PASSES):
+                for t in range(PACK):
+                    for ih in range(I_HALVES):
+                        pt = psum_t.tile([P, PACK, P], BF16, name="pt", tag="t")
+                        for a in range(PACK):
+                            nc.tensor.transpose(
+                                pt[:, a, :], pos_sb[g][:, ih * PACK + a, t * P : (t + 1) * P], ident_bf[:]
+                            )
+                        dst = pos_t[:, g * PACK + t, ih * BANK : (ih + 1) * BANK]
+                        src = pt[:].rearrange("p a i -> p (a i)")
+                        if ih == 0:
+                            nc.vector.tensor_copy(out=dst, in_=src)
+                        else:
+                            nc.scalar.copy(out=dst, in_=src)
+
+            w_grouped = head.tile([P, C * PACK], BF16, name="w_grouped", align_bytes=64)
+            w_grouped_words = w_grouped[:].bitcast(F32).rearrange("p (o u) -> p o u", u=2)
+            for pair in range(O_BLOCKS // 2):
+                pw = psum_t.tile([P, 2, 2 * P], F32, name="pw", tag="t")
+                for u in range(2):
+                    for a in range(2):
+                        nc.tensor.transpose(
+                            pw[:, u, a * P : (a + 1) * P],
+                            w_sb[:, 2 * pair + a, :].bitcast(F32)[:, u * P : (u + 1) * P],
+                            ident_f32[:],
+                        )
+                nc.scalar.copy(
+                    out=w_grouped_words[:, 2 * pair * P : (2 * pair + 2) * P, :],
+                    in_=pw[:].rearrange("p u o -> p o u"),
+                )
+            nc.vector.quantize_mx(out=w_codes[:].bitcast(FP8X4), scales=w_scales[:], in_=w_grouped[:])
+
+        late = stack.enter_context(tc.tile_pool(name="late", bufs=1))
+        store = stack.enter_context(tc.tile_pool(name="store", bufs=4))
+
+        nc.sync.dma_start(
+            out=ped_sb[:].rearrange("p (u e) j -> p u (e j)", u=2),
+            in_=pos_embedding_decoder[0].rearrange("(u p e) h w -> p u (e h w)", u=2, p=P),
+        )
+
+        def load_g(b):
+            gp_sb = g_pool.tile([P, PACK, N], BF16, name="gp_sb")
+            nc.sync.dma_start(
+                out=gp_sb[:].rearrange("p (u e) j -> p u (e j)", u=2),
+                in_=g_proj[b].rearrange("(u p e) j -> p u (e j)", u=2, p=P),
+            )
+            return gp_sb
+
+        def load_x(b):
+            x_sb = late.tile([P, O_BLOCKS, N], BF16, name="x_sb")
+            nc.sync.dma_start(out=x_sb[:], in_=x_rows[b].rearrange("(a p) i -> p a i", p=P))
+            return x_sb
+
+        def quantise_g(gp_sb):
+            g_bf = g_pool.tile([P, PACK, N], BF16, name="g_bf")
+            for t in range(PACK):
+                nc.gpsimd.tensor_tensor(out=g_bf[:, t, :], in0=gp_sb[:, t, :], in1=ped_sb[:, t, :], op=ADD)
+            g_grouped = g_pool.tile([P, J_PASSES, IC, PACK], BF16, name="g_grouped", align_bytes=64)
+            g_codes = codes.tile([P, J_PASSES, IC], U32, name="g_codes", align_bytes=64)
+            g_scales = codes.tile([P, J_PASSES, IC], U8, name="g_scales", align_bytes=64)
+            for g in range(J_PASSES):
+                for half in range(2):
+                    pg = psum_t.tile([P, 2, PACK, P], BF16, name="pg", tag="t")
+                    for a in range(2):
+                        for t in range(PACK):
+                            jb = g * PACK + t
+                            nc.tensor.transpose(
+                                pg[:, a, t, :], g_bf[:, 2 * half + a, jb * P : (jb + 1) * P], ident_bf[:]
+                            )
+                    nc.scalar.copy(
+                        out=g_grouped[:, g, 2 * half * P : (2 * half + 2) * P, :].rearrange(
+                            "p (a c) t -> p a c t", a=2
+                        ),
+                        in_=pg[:].rearrange("p a t c -> p a c t"),
+                    )
+            for g in range(J_PASSES):
+                nc.vector.quantize_mx(
+                    out=g_codes[:, g, :].bitcast(FP8X4),
+                    scales=g_scales[:, g, :],
+                    in_=g_grouped[:, g, :, :].rearrange("p c t -> p (c t)"),
+                )
+            return g_codes, g_scales
+
+        def softmax_block(b, jb, attn_bf):
+            t = jb % PACK
+            s_sb = soft.tile([P, N], F32, name="s_sb")
+            for ih in range(I_HALVES):
+                cols = slice(ih * BANK, (ih + 1) * BANK)
+                acc = psum_s.tile([P, BANK], F32, name="acc")
+                for k in range(IC_CHUNKS):
+                    nc.tensor.matmul(
+                        out=acc[:],
+                        lhsT=phi_sb[b][:, k, jb * P : (jb + 1) * P],
+                        rhs=theta_sb[b][:, k, cols],
+                        start=(k == 0),
+                        stop=(k == IC_CHUNKS - 1),
+                    )
+                nc.vector.tensor_tensor(out=s_sb[:, cols], in0=acc[:], in1=pos_t[:, jb, cols], op=ADD)
+            neg_max = stats.tile([P, 1], F32, name="neg_max")
+            nc.vector.tensor_reduce(out=neg_max[:], in_=s_sb[:], axis=X_AXIS, op=MAX, negate=True)
+            e_sb = soft.tile([P, N], F32, name="e_sb", bufs=3)
+            e_sum = stats.tile([P, 1], F32, name="e_sum")
+            nc.scalar.activation(out=e_sb[:], in_=s_sb[:], func=EXP, bias=neg_max[:], scale=1.0, accum_out=e_sum[:])
+            r_sum = stats.tile([P, 1], F32, name="r_sum")
+            nc.vector.reciprocal(out=r_sum[:], in_=e_sum[:])
+            nc.scalar.activation(out=attn_bf[:, t, :], in_=e_sb[:], func=COPY, scale=r_sum[:])
+
+        def quantise_attn(attn_bf, attn_codes, attn_scales, g):
+            grouped = soft.tile([P, N, PACK], BF16, name="grouped", align_bytes=64)
+            for ih in range(I_HALVES):
+                cols = slice(ih * BANK, (ih + 1) * BANK)
+                nc.vector.tensor_copy(
+                    out=grouped[:, cols, :].rearrange("p (c i) t -> p c t i", i=4),
+                    in_=attn_bf[:, :, cols].rearrange("p t (c i) -> p c t i", i=4),
+                )
+            for ih in range(I_HALVES):
+                cols = slice(ih * BANK, (ih + 1) * BANK)
+                nc.vector.quantize_mx(
+                    out=attn_codes[:, g, cols].bitcast(FP8X4),
+                    scales=attn_scales[:, g, cols],
+                    in_=grouped[:, cols, :].rearrange("p i t -> p (i t)"),
+                )
+
+        def attention(b):
+            attn_codes = codes.tile([P, J_PASSES, N], U32, name="attn_codes", align_bytes=64)
+            attn_scales = codes.tile([P, J_PASSES, N], U8, name="attn_scales", align_bytes=64)
+            for g in range(J_PASSES):
+                attn_bf = soft.tile([P, PACK, N], BF16, name="attn_bf")
+                for t in range(PACK):
+                    softmax_block(b, g * PACK + t, attn_bf)
+                quantise_attn(attn_bf, attn_codes, attn_scales, g)
+            return attn_codes, attn_scales
+
+        def mix_and_project(b, attn_codes, attn_scales, g_codes, g_scales, x_sb):
+            y_grouped = late.tile([P, N, PACK], BF16, name="y_grouped", align_bytes=64)
+            y_codes = late.tile([P, N], U32, name="y_codes", align_bytes=64)
+            y_scales = late.tile([P, N], U8, name="y_scales", align_bytes=64)
+            for ih in range(I_HALVES):
+                for quarter in range(BANK // P):
+                    i_cols = slice(ih * BANK + quarter * P, ih * BANK + (quarter + 1) * P)
+                    yt = psum_t.tile([P, PACK, P], F32, name="yt", tag="t")
+                    for t in range(PACK):
+                        c_cols = slice(t * P, (t + 1) * P)
+                        for g in range(J_PASSES):
+                            nc.tensor.matmul_mx(
+                                out=yt[:, t, :],
+                                lhsT=g_codes[:, g, c_cols].bitcast(FP8X4),
+                                lhsT_scale=g_scales[:, g, c_cols],
+                                rhs=attn_codes[:, g, i_cols].bitcast(FP8X4),
+                                rhs_scale=attn_scales[:, g, i_cols],
+                                start=(g == 0),
+                                stop=(g == J_PASSES - 1),
+                            )
+                    nc.scalar.copy(out=y_grouped[:, i_cols, :], in_=yt[:].rearrange("p t i -> p i t"))
+                cols = slice(ih * BANK, (ih + 1) * BANK)
+                nc.vector.quantize_mx(
+                    out=y_codes[:, cols].bitcast(FP8X4),
+                    scales=y_scales[:, cols],
+                    in_=y_grouped[:, cols, :].rearrange("p i t -> p (i t)"),
+                )
+                for ob in range(O_BLOCKS):
+                    o_cols = slice(ob * P, (ob + 1) * P)
+                    m_acc = psum_m.tile([P, BANK], F32, name="m_acc")
+                    nc.tensor.matmul_mx(
+                        out=m_acc[:],
+                        lhsT=w_codes[:, o_cols].bitcast(FP8X4),
+                        lhsT_scale=w_scales[:, o_cols],
+                        rhs=y_codes[:, cols].bitcast(FP8X4),
+                        rhs_scale=y_scales[:, cols],
+                        start=True,
+                        stop=True,
+                    )
+                    o_sb = store.tile([P, BANK], F32, name="o_sb")
+                    nc.vector.tensor_tensor(out=o_sb[:], in0=m_acc[:], in1=x_sb[:, ob, cols], op=ADD)
+                    nc.sync.dma_start(out=out_rows[b, o_cols, cols], in_=o_sb[:])
+
+        gp_sb = load_g(0)
+        load_theta(1)
+        load_phi(1, 0)
+        load_phi(1, 1)
+        x_sb = load_x(0)
+        for b in range(B):
+            g_codes, g_scales = quantise_g(gp_sb)
+            if b + 1 < B:
+                gp_sb = load_g(b + 1)
+            attn_codes, attn_scales = attention(b)
+            mix_and_project(b, attn_codes, attn_scales, g_codes, g_scales, x_sb)
+            if b + 1 < B:
+                x_sb = load_x(b + 1)

@@ -10,6 +10,7 @@ U8 = mybir.dt.uint8
 FP8X4 = mybir.dt.float8_e4m3fn_x4
 ADD = mybir.AluOpType.add
 MAX = mybir.AluOpType.max
+MULT = mybir.AluOpType.mult
 EXP = mybir.ActivationFunctionType.Exp
 COPY = mybir.ActivationFunctionType.Copy
 X_AXIS = mybir.AxisListType.X
@@ -27,6 +28,10 @@ J_BLOCKS = N // P
 I_HALVES = N // BANK
 IC_CHUNKS = IC // P
 O_BLOCKS = C // P
+I_BLOCKS = N // P
+BANK_BLOCKS = BANK // P
+SLOTS = B * J_BLOCKS
+S_BANKS = SLOTS * I_HALVES
 
 FLOPS = 3 * 2 * B * N * N * IC
 
@@ -41,13 +46,15 @@ def tile_nonlocalblock_pa_kernel(
     with ExitStack() as stack:
         const = stack.enter_context(tc.tile_pool(name="const", bufs=1))
         inputs = stack.enter_context(tc.tile_pool(name="inputs", bufs=2))
-        g_pool = stack.enter_context(tc.tile_pool(name="g_pool", bufs=1))
         soft = stack.enter_context(tc.tile_pool(name="soft", bufs=2))
-        stats = stack.enter_context(tc.tile_pool(name="stats", bufs=8))
+        stats = stack.enter_context(tc.tile_pool(name="stats", bufs=6))
         codes = stack.enter_context(tc.tile_pool(name="codes", bufs=2))
-        psum_s = stack.enter_context(tc.psum_pool(name="psum_s", bufs=3))
-        psum_t = stack.enter_context(tc.psum_pool(name="psum_t", bufs=3))
+        late = stack.enter_context(tc.tile_pool(name="late", bufs=1))
+        store = stack.enter_context(tc.tile_pool(name="store", bufs=8))
+        psum_acc = stack.enter_context(tc.psum_pool(name="psum_acc", bufs=4))
         psum_m = stack.enter_context(tc.psum_pool(name="psum_m", bufs=2))
+        psum_tp = stack.enter_context(tc.psum_pool(name="psum_tp", bufs=2))
+        stack.enter_context(tc.manual_schedule())
 
         ident_bf = const.tile([P, P], BF16, name="ident_bf")
         make_identity(nc, ident_bf[:])
@@ -56,229 +63,364 @@ def tile_nonlocalblock_pa_kernel(
 
         theta_sb = []
         phi_sb = []
+        gp_sb = []
         for b in range(B):
-            theta_sb.append(inputs.tile([P, IC_CHUNKS, N], BF16, name="theta_sb", tag="theta"))
-            phi_sb.append(inputs.tile([P, IC_CHUNKS, N], BF16, name="phi_sb", tag="phi"))
+            theta_sb.append([inputs.tile([P, IC_CHUNKS, BANK], BF16, name="theta_sb", tag="theta%d" % h) for h in range(2)])
+            phi_sb.append([inputs.tile([P, IC_CHUNKS, K_PASS], BF16, name="phi_sb", tag="phi%d" % h) for h in range(2)])
+            gp_sb.append(inputs.tile([P, PACK, N], BF16, name="gp_sb", tag="gp"))
+        pos_sb = []
+        for g in range(J_PASSES):
+            pos_sb.append(
+                [late.tile([P, BANK_BLOCKS, K_PASS], BF16, name="pos_sb", tag="pos%d" % (2 * g + ih)) for ih in range(2)]
+            )
+        ped_sb = const.tile([P, PACK, N], BF16, name="ped_sb")
+        w_sb = late.tile([P, O_BLOCKS, IC], BF16, name="w_sb", tag="y_grouped", align_bytes=64)
 
-        def load_theta(b):
-            nc.sync.dma_start(out=theta_sb[b][:], in_=theta[b].rearrange("(k p) i -> p k i", p=P))
+        def load_theta(b, ih):
+            cols = slice(ih * BANK, (ih + 1) * BANK)
+            nc.sync.dma_start(
+                out=theta_sb[b][ih][:], in_=theta[b, :, cols].rearrange("(k p) i -> p k i", p=P)
+            )
 
         def load_phi(b, g):
             cols = slice(g * K_PASS, (g + 1) * K_PASS)
             nc.sync.dma_start(
-                out=phi_sb[b][:, :, cols], in_=phi[b, :, cols].rearrange("(k p) j -> p k j", p=P)
+                out=phi_sb[b][g][:], in_=phi[b, :, cols].rearrange("(k p) j -> p k j", p=P)
             )
 
-        pos_t = const.tile([P, J_BLOCKS, N], BF16, name="pos_t")
-        w_codes = const.tile([P, C], U32, name="w_codes", align_bytes=64)
-        w_scales = const.tile([P, C], U8, name="w_scales", align_bytes=64)
-        ped_sb = const.tile([P, PACK, N], BF16, name="ped_sb")
+        def load_pos(g, ih):
+            cols = slice(g * K_PASS, (g + 1) * K_PASS)
+            rows = slice(ih * BANK, (ih + 1) * BANK)
+            nc.sync.dma_start(
+                out=pos_sb[g][ih][:],
+                in_=pos_embedding[0, rows, cols].rearrange("(a p) j -> p a j", p=P),
+            )
 
-        with tc.tile_pool(name="head", bufs=1) as head:
-            pos_sb = []
-            for g in range(J_PASSES):
-                pos_sb.append(head.tile([P, J_BLOCKS, K_PASS], BF16, name="pos_sb%d" % g))
+        def load_g(b):
+            nc.sync.dma_start(
+                out=gp_sb[b][:].rearrange("p (u e) j -> p u (e j)", u=2),
+                in_=g_proj[b].rearrange("(u p e) j -> p u (e j)", u=2, p=P),
+            )
 
-            def load_pos(g):
-                cols = slice(g * K_PASS, (g + 1) * K_PASS)
-                nc.sync.dma_start(
-                    out=pos_sb[g][:], in_=pos_embedding[0, :, cols].rearrange("(a p) j -> p a j", p=P)
-                )
+        def load_x(b):
+            quarters = []
+            for q in range(4):
+                if b == 0:
+                    x_q = late.tile([P, O_BLOCKS // 4, N], BF16, name="x_q", tag="pos%d" % q)
+                else:
+                    x_q = inputs.tile([P, O_BLOCKS // 4, N], BF16, name="x_q", tag=("theta0", "theta1", "phi0", "phi1")[q])
+                rows = slice(q * (C // 4), (q + 1) * (C // 4))
+                nc.sync.dma_start(out=x_q[:], in_=x_rows[b, rows, :].rearrange("(a p) i -> p a i", p=P))
+                quarters.append(x_q)
+            return quarters
 
-            load_pos(0)
-            load_theta(0)
-            load_phi(0, 0)
-            load_pos(1)
-            load_phi(0, 1)
-            w_sb = head.tile([P, O_BLOCKS, IC], BF16, name="w_sb")
-            nc.sync.dma_start(out=w_sb[:], in_=w_mask.rearrange("(a p) c -> p a c", p=P))
-
-            for g in range(J_PASSES):
-                for t in range(PACK):
-                    for ih in range(I_HALVES):
-                        pt = psum_t.tile([P, PACK, P], BF16, name="pt", tag="t")
-                        for a in range(PACK):
-                            nc.tensor.transpose(
-                                pt[:, a, :], pos_sb[g][:, ih * PACK + a, t * P : (t + 1) * P], ident_bf[:]
-                            )
-                        dst = pos_t[:, g * PACK + t, ih * BANK : (ih + 1) * BANK]
-                        src = pt[:].rearrange("p a i -> p (a i)")
-                        if ih == 0:
-                            nc.vector.tensor_copy(out=dst, in_=src)
-                        else:
-                            nc.scalar.copy(out=dst, in_=src)
-
-            w_grouped = head.tile([P, C * PACK], BF16, name="w_grouped", align_bytes=64)
-            w_grouped_words = w_grouped[:].bitcast(F32).rearrange("p (o u) -> p o u", u=2)
-            for pair in range(O_BLOCKS // 2):
-                pw = psum_t.tile([P, 2, 2 * P], F32, name="pw", tag="t")
-                for u in range(2):
-                    for a in range(2):
-                        nc.tensor.transpose(
-                            pw[:, u, a * P : (a + 1) * P],
-                            w_sb[:, 2 * pair + a, :].bitcast(F32)[:, u * P : (u + 1) * P],
-                            ident_f32[:],
-                        )
-                nc.scalar.copy(
-                    out=w_grouped_words[:, 2 * pair * P : (2 * pair + 2) * P, :],
-                    in_=pw[:].rearrange("p u o -> p o u"),
-                )
-            nc.vector.quantize_mx(out=w_codes[:].bitcast(FP8X4), scales=w_scales[:], in_=w_grouped[:])
-
-        late = stack.enter_context(tc.tile_pool(name="late", bufs=1))
-        store = stack.enter_context(tc.tile_pool(name="store", bufs=4))
-
+        load_theta(0, 0)
+        load_phi(0, 0)
+        load_pos(0, 0)
+        load_theta(0, 1)
+        load_pos(0, 1)
+        load_phi(0, 1)
+        load_pos(1, 0)
+        load_pos(1, 1)
         nc.sync.dma_start(
             out=ped_sb[:].rearrange("p (u e) j -> p u (e j)", u=2),
             in_=pos_embedding_decoder[0].rearrange("(u p e) h w -> p u (e h w)", u=2, p=P),
         )
+        load_g(0)
+        load_g(1)
+        nc.sync.dma_start(out=w_sb[:], in_=w_mask.rearrange("(a p) c -> p a c", p=P))
+        for ih in range(I_HALVES):
+            load_theta(1, ih)
+        for g in range(J_PASSES):
+            load_phi(1, g)
 
-        def load_g(b):
-            gp_sb = g_pool.tile([P, PACK, N], BF16, name="gp_sb")
-            nc.sync.dma_start(
-                out=gp_sb[:].rearrange("p (u e) j -> p u (e j)", u=2),
-                in_=g_proj[b].rearrange("(u p e) j -> p u (e j)", u=2, p=P),
-            )
-            return gp_sb
-
-        def load_x(b):
-            x_sb = late.tile([P, O_BLOCKS, N], BF16, name="x_sb")
-            nc.sync.dma_start(out=x_sb[:], in_=x_rows[b].rearrange("(a p) i -> p a i", p=P))
-            return x_sb
-
-        def quantise_g(gp_sb):
-            g_bf = g_pool.tile([P, PACK, N], BF16, name="g_bf")
+        pos_f32 = const.tile([P, J_BLOCKS, I_BLOCKS, P], F32, name="pos_f32")
+        for ih in range(I_HALVES):
+            blocks = slice(ih * BANK_BLOCKS, (ih + 1) * BANK_BLOCKS)
             for t in range(PACK):
-                nc.gpsimd.tensor_tensor(out=g_bf[:, t, :], in0=gp_sb[:, t, :], in1=ped_sb[:, t, :], op=ADD)
-            g_grouped = g_pool.tile([P, J_PASSES, IC, PACK], BF16, name="g_grouped", align_bytes=64)
-            g_codes = codes.tile([P, J_PASSES, IC], U32, name="g_codes", align_bytes=64)
-            g_scales = codes.tile([P, J_PASSES, IC], U8, name="g_scales", align_bytes=64)
-            for g in range(J_PASSES):
-                for half in range(2):
-                    pg = psum_t.tile([P, 2, PACK, P], BF16, name="pg", tag="t")
-                    for a in range(2):
-                        for t in range(PACK):
-                            jb = g * PACK + t
-                            nc.tensor.transpose(
-                                pg[:, a, t, :], g_bf[:, 2 * half + a, jb * P : (jb + 1) * P], ident_bf[:]
-                            )
-                    nc.scalar.copy(
-                        out=g_grouped[:, g, 2 * half * P : (2 * half + 2) * P, :].rearrange(
-                            "p (a c) t -> p a c t", a=2
-                        ),
-                        in_=pg[:].rearrange("p a t c -> p a c t"),
-                    )
-            for g in range(J_PASSES):
-                nc.vector.quantize_mx(
-                    out=g_codes[:, g, :].bitcast(FP8X4),
-                    scales=g_scales[:, g, :],
-                    in_=g_grouped[:, g, :, :].rearrange("p c t -> p (c t)"),
-                )
-            return g_codes, g_scales
+                nc.vector.tensor_copy(out=pos_f32[:, t, blocks, :], in_=pos_sb[0][ih][:, :, t * P : (t + 1) * P])
+        for t in range(PACK):
+          for ih in range(I_HALVES):
+            nc.gpsimd.tensor_scalar(
+                out=pos_f32[:, PACK + t, ih * BANK_BLOCKS : (ih + 1) * BANK_BLOCKS, :],
+                in0=pos_sb[1][ih][:, :, t * P : (t + 1) * P],
+                scalar1=1.0,
+                scalar2=0.0,
+                op0=MULT,
+                op1=ADD,
+            )
+        x_sb = [load_x(0)]
+        for b in range(B):
+            for t in range(PACK):
+                nc.gpsimd.tensor_tensor(out=gp_sb[b][:, t, :], in0=gp_sb[b][:, t, :], in1=ped_sb[:, t, :], op=ADD)
 
-        def softmax_block(b, jb, attn_bf):
-            t = jb % PACK
-            s_sb = soft.tile([P, N], F32, name="s_sb")
-            for ih in range(I_HALVES):
-                cols = slice(ih * BANK, (ih + 1) * BANK)
-                acc = psum_s.tile([P, BANK], F32, name="acc")
-                for k in range(IC_CHUNKS):
+        acc = {}
+        bank_max = {}
+        bank_sum = {}
+        e_sb = {}
+        attn_bf = {}
+        grouped = {}
+        attn_codes = []
+        attn_scales = []
+        g_grouped = {}
+        g_codes = []
+        g_scales = []
+        for b in range(B):
+            attn_codes.append(codes.tile([P, J_PASSES, N], U32, name="attn_codes", align_bytes=64))
+            attn_scales.append(codes.tile([P, J_PASSES, N], U8, name="attn_scales", align_bytes=64))
+            g_codes.append(codes.tile([P, J_PASSES, IC], U32, name="g_codes", align_bytes=64))
+            g_scales.append(codes.tile([P, J_PASSES, IC], U8, name="g_scales", align_bytes=64))
+        w_grouped = const.tile([P, C * PACK], BF16, name="w_grouped", align_bytes=64)
+        w_codes = const.tile([P, C], U32, name="w_codes", align_bytes=64)
+        w_scales = const.tile([P, C], U8, name="w_scales", align_bytes=64)
+        y_grouped = {}
+        y_codes = {}
+        y_scales = {}
+        tp_tiles = {}
+
+        def add_pos(m, a):
+            n, ih = divmod(m, I_HALVES)
+            nc.tensor.matmul(
+                out=acc[m][:, a * P : (a + 1) * P],
+                lhsT=pos_f32[:, n % J_BLOCKS, ih * BANK_BLOCKS + a, :],
+                rhs=ident_f32[:],
+                start=False,
+                stop=(a == BANK_BLOCKS - 1),
+                is_transpose=True,
+            )
+
+        def scores_bank(m):
+            n, ih = divmod(m, I_HALVES)
+            b, jb = divmod(n, J_BLOCKS)
+            if m < S_BANKS:
+                acc[m] = psum_acc.tile([P, BANK], F32, name="acc")
+            for k in range(IC_CHUNKS):
+                if m < S_BANKS:
                     nc.tensor.matmul(
-                        out=acc[:],
-                        lhsT=phi_sb[b][:, k, jb * P : (jb + 1) * P],
-                        rhs=theta_sb[b][:, k, cols],
+                        out=acc[m][:],
+                        lhsT=phi_sb[b][jb // PACK][:, k, (jb % PACK) * P : (jb % PACK + 1) * P],
+                        rhs=theta_sb[b][ih][:, k, :],
                         start=(k == 0),
-                        stop=(k == IC_CHUNKS - 1),
+                        stop=False,
                     )
-                nc.vector.tensor_tensor(out=s_sb[:, cols], in0=acc[:], in1=pos_t[:, jb, cols], op=ADD)
+                if m >= 1:
+                    add_pos(m - 1, k)
+
+        def bank_maximum(m):
+            n, ih = divmod(m, I_HALVES)
+            if ih == 0:
+                bank_max[n] = stats.tile([P, I_HALVES], F32, name="bank_max")
+            nc.vector.tensor_reduce(out=bank_max[n][:, ih : ih + 1], in_=acc[m][:], axis=X_AXIS, op=MAX)
+
+        def exponentials(n):
             neg_max = stats.tile([P, 1], F32, name="neg_max")
-            nc.vector.tensor_reduce(out=neg_max[:], in_=s_sb[:], axis=X_AXIS, op=MAX, negate=True)
-            e_sb = soft.tile([P, N], F32, name="e_sb", bufs=3)
+            nc.vector.tensor_reduce(out=neg_max[:], in_=bank_max[n][:], axis=X_AXIS, op=MAX, negate=True)
+            e_sb[n] = soft.tile([P, N], F32, name="e_sb", bufs=3)
+            bank_sum[n] = stats.tile([P, I_HALVES], F32, name="bank_sum")
+            for ih in range(I_HALVES):
+                nc.scalar.activation(
+                    out=e_sb[n][:, ih * BANK : (ih + 1) * BANK],
+                    in_=acc[n * I_HALVES + ih][:],
+                    func=EXP,
+                    bias=neg_max[:],
+                    scale=1.0,
+                    accum_out=bank_sum[n][:, ih : ih + 1],
+                )
+
+        def normalise(n):
+            r, t = divmod(n, PACK)
+            if t == 0:
+                attn_bf[r] = soft.tile([P, PACK, N], BF16, name="attn_bf")
             e_sum = stats.tile([P, 1], F32, name="e_sum")
-            nc.scalar.activation(out=e_sb[:], in_=s_sb[:], func=EXP, bias=neg_max[:], scale=1.0, accum_out=e_sum[:])
+            nc.vector.tensor_reduce(out=e_sum[:], in_=bank_sum[n][:], axis=X_AXIS, op=ADD)
             r_sum = stats.tile([P, 1], F32, name="r_sum")
             nc.vector.reciprocal(out=r_sum[:], in_=e_sum[:])
-            nc.scalar.activation(out=attn_bf[:, t, :], in_=e_sb[:], func=COPY, scale=r_sum[:])
-
-        def quantise_attn(attn_bf, attn_codes, attn_scales, g):
-            grouped = soft.tile([P, N, PACK], BF16, name="grouped", align_bytes=64)
-            for ih in range(I_HALVES):
-                cols = slice(ih * BANK, (ih + 1) * BANK)
-                nc.vector.tensor_copy(
-                    out=grouped[:, cols, :].rearrange("p (c i) t -> p c t i", i=4),
-                    in_=attn_bf[:, :, cols].rearrange("p t (c i) -> p c t i", i=4),
+            if n % 2 == 1:
+                nc.vector.tensor_scalar(
+                    out=attn_bf[r][:, t, :], in0=e_sb[n][:], scalar1=r_sum[:], scalar2=None, op0=MULT
                 )
-            for ih in range(I_HALVES):
-                cols = slice(ih * BANK, (ih + 1) * BANK)
-                nc.vector.quantize_mx(
-                    out=attn_codes[:, g, cols].bitcast(FP8X4),
-                    scales=attn_scales[:, g, cols],
-                    in_=grouped[:, cols, :].rearrange("p i t -> p (i t)"),
-                )
+            else:
+                nc.scalar.activation(out=attn_bf[r][:, t, :], in_=e_sb[n][:], func=COPY, scale=r_sum[:])
 
-        def attention(b):
-            attn_codes = codes.tile([P, J_PASSES, N], U32, name="attn_codes", align_bytes=64)
-            attn_scales = codes.tile([P, J_PASSES, N], U8, name="attn_scales", align_bytes=64)
-            for g in range(J_PASSES):
-                attn_bf = soft.tile([P, PACK, N], BF16, name="attn_bf")
+        def regroup(r, ih):
+            if ih == 0:
+                grouped[r] = soft.tile([P, N, PACK], BF16, name="grouped", align_bytes=64)
+            cols = slice(ih * BANK, (ih + 1) * BANK)
+            nc.vector.tensor_copy(
+                out=grouped[r][:, cols, :].rearrange("p (c i) t -> p c t i", i=4),
+                in_=attn_bf[r][:, :, cols].rearrange("p t (c i) -> p c t i", i=4),
+            )
+
+        def quantise_attn(r, ih):
+            b, g = divmod(r, J_PASSES)
+            cols = slice(ih * BANK, (ih + 1) * BANK)
+            nc.vector.quantize_mx(
+                out=attn_codes[b][:, g, cols].bitcast(FP8X4),
+                scales=attn_scales[b][:, g, cols],
+                in_=grouped[r][:, cols, :].rearrange("p i t -> p (i t)"),
+            )
+
+        def g_tile(b, k):
+            half, g = divmod(k, J_PASSES)
+            if k == 0:
+                g_grouped[b] = soft.tile([P, J_PASSES, IC, PACK], BF16, name="g_grouped", bufs=1, align_bytes=64)
+            pg = psum_tp.tile([P, 2, PACK, P], BF16, name="pg", tag="tp")
+            tp_tiles["g", b, k] = pg
+            for a in range(2):
                 for t in range(PACK):
-                    softmax_block(b, g * PACK + t, attn_bf)
-                quantise_attn(attn_bf, attn_codes, attn_scales, g)
-            return attn_codes, attn_scales
+                    jb = g * PACK + t
+                    nc.tensor.transpose(pg[:, a, t, :], gp_sb[b][:, 2 * half + a, jb * P : (jb + 1) * P], ident_bf[:])
 
-        def mix_and_project(b, attn_codes, attn_scales, g_codes, g_scales, x_sb):
-            y_grouped = late.tile([P, N, PACK], BF16, name="y_grouped", align_bytes=64)
-            y_codes = late.tile([P, N], U32, name="y_codes", align_bytes=64)
-            y_scales = late.tile([P, N], U8, name="y_scales", align_bytes=64)
-            for ih in range(I_HALVES):
-                for quarter in range(BANK // P):
-                    i_cols = slice(ih * BANK + quarter * P, ih * BANK + (quarter + 1) * P)
-                    yt = psum_t.tile([P, PACK, P], F32, name="yt", tag="t")
-                    for t in range(PACK):
-                        c_cols = slice(t * P, (t + 1) * P)
-                        for g in range(J_PASSES):
-                            nc.tensor.matmul_mx(
-                                out=yt[:, t, :],
-                                lhsT=g_codes[:, g, c_cols].bitcast(FP8X4),
-                                lhsT_scale=g_scales[:, g, c_cols],
-                                rhs=attn_codes[:, g, i_cols].bitcast(FP8X4),
-                                rhs_scale=attn_scales[:, g, i_cols],
-                                start=(g == 0),
-                                stop=(g == J_PASSES - 1),
-                            )
-                    nc.scalar.copy(out=y_grouped[:, i_cols, :], in_=yt[:].rearrange("p t i -> p i t"))
-                cols = slice(ih * BANK, (ih + 1) * BANK)
-                nc.vector.quantize_mx(
-                    out=y_codes[:, cols].bitcast(FP8X4),
-                    scales=y_scales[:, cols],
-                    in_=y_grouped[:, cols, :].rearrange("p i t -> p (i t)"),
-                )
-                for ob in range(O_BLOCKS):
-                    o_cols = slice(ob * P, (ob + 1) * P)
-                    m_acc = psum_m.tile([P, BANK], F32, name="m_acc")
-                    nc.tensor.matmul_mx(
-                        out=m_acc[:],
-                        lhsT=w_codes[:, o_cols].bitcast(FP8X4),
-                        lhsT_scale=w_scales[:, o_cols],
-                        rhs=y_codes[:, cols].bitcast(FP8X4),
-                        rhs_scale=y_scales[:, cols],
-                        start=True,
-                        stop=True,
+        def g_tile_out(b, k):
+            half, g = divmod(k, J_PASSES)
+            nc.scalar.copy(
+                out=g_grouped[b][:, g, 2 * half * P : (2 * half + 2) * P, :].rearrange("p (a c) t -> p a c t", a=2),
+                in_=tp_tiles["g", b, k][:].rearrange("p a t c -> p a c t"),
+            )
+
+        def g_quantise(b, g):
+            nc.vector.quantize_mx(
+                out=g_codes[b][:, g, :].bitcast(FP8X4),
+                scales=g_scales[b][:, g, :],
+                in_=g_grouped[b][:, g, :, :].rearrange("p c t -> p (c t)"),
+            )
+
+        def w_tile(k):
+            pw = psum_tp.tile([P, 2, 2 * P], F32, name="pw", tag="tp")
+            tp_tiles["w", k] = pw
+            for u in range(2):
+                for a in range(2):
+                    nc.tensor.transpose(
+                        pw[:, u, a * P : (a + 1) * P],
+                        w_sb[:, 2 * k + a, :].bitcast(F32)[:, u * P : (u + 1) * P],
+                        ident_f32[:],
                     )
-                    o_sb = store.tile([P, BANK], F32, name="o_sb")
-                    nc.vector.tensor_tensor(out=o_sb[:], in0=m_acc[:], in1=x_sb[:, ob, cols], op=ADD)
-                    nc.sync.dma_start(out=out_rows[b, o_cols, cols], in_=o_sb[:])
 
-        gp_sb = load_g(0)
-        load_theta(1)
-        load_phi(1, 0)
-        load_phi(1, 1)
-        x_sb = load_x(0)
-        for b in range(B):
-            g_codes, g_scales = quantise_g(gp_sb)
+        def w_tile_out(k):
+            words = w_grouped[:].bitcast(F32).rearrange("p (o u) -> p o u", u=2)
+            nc.scalar.copy(
+                out=words[:, 2 * k * P : (2 * k + 2) * P, :], in_=tp_tiles["w", k][:].rearrange("p u o -> p o u")
+            )
+
+        def y_chunk(b, ic):
+            if ic == 0:
+                y_grouped[b] = late.tile([P, N, PACK], BF16, name="y_grouped", align_bytes=64)
+            i_cols = slice(ic * P, (ic + 1) * P)
+            yt = psum_tp.tile([P, PACK, P], F32, name="yt", tag="tp")
+            tp_tiles["y", b, ic] = yt
+            for t in range(PACK):
+                c_cols = slice(t * P, (t + 1) * P)
+                for g in range(J_PASSES):
+                    nc.tensor.matmul_mx(
+                        out=yt[:, t, :],
+                        lhsT=g_codes[b][:, g, c_cols].bitcast(FP8X4),
+                        lhsT_scale=g_scales[b][:, g, c_cols],
+                        rhs=attn_codes[b][:, g, i_cols].bitcast(FP8X4),
+                        rhs_scale=attn_scales[b][:, g, i_cols],
+                        start=(g == 0),
+                        stop=(g == J_PASSES - 1),
+                    )
+
+        def y_chunk_out(b, ic):
+            nc.scalar.copy(
+                out=y_grouped[b][:, ic * P : (ic + 1) * P, :], in_=tp_tiles["y", b, ic][:].rearrange("p t i -> p i t")
+            )
+
+        def y_quantise(b, ih):
+            if ih == 0:
+                y_codes[b] = late.tile([P, N], U32, name="y_codes", align_bytes=64)
+                y_scales[b] = late.tile([P, N], U8, name="y_scales", align_bytes=64)
+            cols = slice(ih * BANK, (ih + 1) * BANK)
+            nc.vector.quantize_mx(
+                out=y_codes[b][:, cols].bitcast(FP8X4),
+                scales=y_scales[b][:, cols],
+                in_=y_grouped[b][:, cols, :].rearrange("p i t -> p (i t)"),
+            )
+
+        def m_tile(b, ih, ob):
+            cols = slice(ih * BANK, (ih + 1) * BANK)
+            o_cols = slice(ob * P, (ob + 1) * P)
             if b + 1 < B:
-                gp_sb = load_g(b + 1)
-            attn_codes, attn_scales = attention(b)
-            mix_and_project(b, attn_codes, attn_scales, g_codes, g_scales, x_sb)
-            if b + 1 < B:
-                x_sb = load_x(b + 1)
+                m_acc = psum_m.tile([P, BANK], F32, name="m_acc")
+            else:
+                m_acc = psum_acc.tile([P, BANK], F32, name="m_acc", tag="acc")
+            tp_tiles["m", b, ih, ob] = m_acc
+            nc.tensor.matmul_mx(
+                out=m_acc[:],
+                lhsT=w_codes[:, o_cols].bitcast(FP8X4),
+                lhsT_scale=w_scales[:, o_cols],
+                rhs=y_codes[b][:, cols].bitcast(FP8X4),
+                rhs_scale=y_scales[b][:, cols],
+                start=True,
+                stop=True,
+            )
+
+        def m_tile_out(b, ih, ob):
+            cols = slice(ih * BANK, (ih + 1) * BANK)
+            o_cols = slice(ob * P, (ob + 1) * P)
+            o_sb = store.tile([P, BANK], F32, name="o_sb")
+            nc.vector.tensor_tensor(out=o_sb[:], in0=tp_tiles["m", b, ih, ob][:], in1=x_sb[b][ob // 2][:, ob % 2, cols], op=ADD)
+            nc.sync.dma_start(out=out_rows[b, o_cols, cols], in_=o_sb[:])
+
+        def background_tensor(n):
+            b, k = divmod(n - 4, PACK)
+            if 0 <= b < B:
+                g_tile(b, k)
+            if 0 <= n - 5 < O_BLOCKS // 2:
+                w_tile(n - 5)
+            b, k = divmod(n - 11, J_BLOCKS)
+            if 0 <= b < B and k < 4:
+                y_chunk(b, 2 * k)
+                y_chunk(b, 2 * k + 1)
+            b, k = divmod(n - 15, J_BLOCKS)
+            if 0 <= b < B and k < 16 // 2:
+                for tile_no in range(2 * k, 2 * k + 2):
+                    m_tile(b, tile_no // O_BLOCKS, tile_no % O_BLOCKS)
+
+        def background_out(n):
+            b, k = divmod(n - 4, PACK)
+            if 0 <= b < B:
+                g_tile_out(b, k)
+            if 0 <= n - 5 < O_BLOCKS // 2:
+                w_tile_out(n - 5)
+            b, k = divmod(n - 11, J_BLOCKS)
+            if 0 <= b < B and k < 4:
+                y_chunk_out(b, 2 * k)
+                y_chunk_out(b, 2 * k + 1)
+            b, k = divmod(n - 15, J_BLOCKS)
+            if 0 <= b < B and k < 16 // 2:
+                for tile_no in range(2 * k, 2 * k + 2):
+                    m_tile_out(b, tile_no // O_BLOCKS, tile_no % O_BLOCKS)
+
+        def background_quantise(n):
+            r, k = divmod(n - 5, PACK)
+            if 0 <= r < B * J_PASSES:
+                if k < I_HALVES:
+                    regroup(r, k)
+                if 1 <= k < 1 + I_HALVES:
+                    quantise_attn(r, k - 1)
+            b, k = divmod(n - 4 - 4, PACK)
+            if 0 <= b < B and k < J_PASSES:
+                g_quantise(b, k)
+            if n - 5 == O_BLOCKS // 2 + 1:
+                nc.vector.quantize_mx(out=w_codes[:].bitcast(FP8X4), scales=w_scales[:], in_=w_grouped[:])
+            b, k = divmod(n - 11 - 3, J_BLOCKS)
+            if 0 <= b < B and (k == 0 or k == 2):
+                y_quantise(b, k // 2)
+
+        for n in range(34):
+            if 2 * n <= S_BANKS:
+                scores_bank(2 * n)
+            background_out(n - 1)
+            if 1 <= n <= SLOTS:
+                bank_maximum(2 * n - 1)
+                exponentials(n - 1)
+            if n < SLOTS:
+                scores_bank(2 * n + 1)
+                bank_maximum(2 * n)
+            if 2 <= n < SLOTS + 2:
+                normalise(n - 2)
+            background_quantise(n)
+            background_tensor(n)
+            if n == 10:
+                x_sb.append(load_x(1))

@@ -54,7 +54,6 @@ def tile_nonlocalblock_pa_kernel(
         psum_acc = stack.enter_context(tc.psum_pool(name="psum_acc", bufs=4))
         psum_m = stack.enter_context(tc.psum_pool(name="psum_m", bufs=2))
         psum_tp = stack.enter_context(tc.psum_pool(name="psum_tp", bufs=2))
-        stack.enter_context(tc.manual_schedule())
 
         ident_bf = const.tile([P, P], BF16, name="ident_bf")
         make_identity(nc, ident_bf[:])
@@ -189,22 +188,23 @@ def tile_nonlocalblock_pa_kernel(
                 is_transpose=True,
             )
 
-        def scores_bank(m):
-            n, ih = divmod(m, I_HALVES)
+        def scores(n):
             b, jb = divmod(n, J_BLOCKS)
-            if m < S_BANKS:
+            g, t = divmod(jb, PACK)
+            for ih in range(I_HALVES):
+                m = n * I_HALVES + ih
                 acc[m] = psum_acc.tile([P, BANK], F32, name="acc")
-            for k in range(IC_CHUNKS):
-                if m < S_BANKS:
+                for k in range(IC_CHUNKS):
                     nc.tensor.matmul(
                         out=acc[m][:],
-                        lhsT=phi_sb[b][jb // PACK][:, k, (jb % PACK) * P : (jb % PACK + 1) * P],
+                        lhsT=phi_sb[b][g][:, k, t * P : (t + 1) * P],
                         rhs=theta_sb[b][ih][:, k, :],
                         start=(k == 0),
                         stop=False,
                     )
-                if m >= 1:
-                    add_pos(m - 1, k)
+            for ih in range(I_HALVES):
+                for a in range(BANK_BLOCKS):
+                    add_pos(n * I_HALVES + ih, a)
 
         def bank_maximum(m):
             n, ih = divmod(m, I_HALVES)
@@ -368,11 +368,11 @@ def tile_nonlocalblock_pa_kernel(
                 g_tile(b, k)
             if 0 <= n - 5 < O_BLOCKS // 2:
                 w_tile(n - 5)
-            b, k = divmod(n - 11, J_BLOCKS)
+            b, k = divmod(n - 10, J_BLOCKS)
             if 0 <= b < B and k < 4:
                 y_chunk(b, 2 * k)
                 y_chunk(b, 2 * k + 1)
-            b, k = divmod(n - 15, J_BLOCKS)
+            b, k = divmod(n - 14, J_BLOCKS)
             if 0 <= b < B and k < 16 // 2:
                 for tile_no in range(2 * k, 2 * k + 2):
                     m_tile(b, tile_no // O_BLOCKS, tile_no % O_BLOCKS)
@@ -383,17 +383,17 @@ def tile_nonlocalblock_pa_kernel(
                 g_tile_out(b, k)
             if 0 <= n - 5 < O_BLOCKS // 2:
                 w_tile_out(n - 5)
-            b, k = divmod(n - 11, J_BLOCKS)
+            b, k = divmod(n - 10, J_BLOCKS)
             if 0 <= b < B and k < 4:
                 y_chunk_out(b, 2 * k)
                 y_chunk_out(b, 2 * k + 1)
-            b, k = divmod(n - 15, J_BLOCKS)
+            b, k = divmod(n - 14, J_BLOCKS)
             if 0 <= b < B and k < 16 // 2:
                 for tile_no in range(2 * k, 2 * k + 2):
                     m_tile_out(b, tile_no // O_BLOCKS, tile_no % O_BLOCKS)
 
         def background_quantise(n):
-            r, k = divmod(n - 5, PACK)
+            r, k = divmod(n - 4, PACK)
             if 0 <= r < B * J_PASSES:
                 if k < I_HALVES:
                     regroup(r, k)
@@ -404,22 +404,20 @@ def tile_nonlocalblock_pa_kernel(
                 g_quantise(b, k)
             if n - 5 == O_BLOCKS // 2 + 1:
                 nc.vector.quantize_mx(out=w_codes[:].bitcast(FP8X4), scales=w_scales[:], in_=w_grouped[:])
-            b, k = divmod(n - 11 - 3, J_BLOCKS)
+            b, k = divmod(n - 10 - 3, J_BLOCKS)
             if 0 <= b < B and (k == 0 or k == 2):
                 y_quantise(b, k // 2)
 
         for n in range(34):
-            if 2 * n <= S_BANKS:
-                scores_bank(2 * n)
-            background_out(n - 1)
-            if 1 <= n <= SLOTS:
-                bank_maximum(2 * n - 1)
-                exponentials(n - 1)
             if n < SLOTS:
-                scores_bank(2 * n + 1)
+                scores(n)
+            background_out(n - 1)
+            if n < SLOTS:
                 bank_maximum(2 * n)
-            if 2 <= n < SLOTS + 2:
-                normalise(n - 2)
+                bank_maximum(2 * n + 1)
+                exponentials(n)
+            if 1 <= n < SLOTS + 1:
+                normalise(n - 1)
             background_quantise(n)
             background_tensor(n)
             if n == 10:

@@ -51,8 +51,7 @@ def tile_nonlocalblock_pa_kernel(
         codes = stack.enter_context(tc.tile_pool(name="codes", bufs=2))
         late = stack.enter_context(tc.tile_pool(name="late", bufs=1))
         store = stack.enter_context(tc.tile_pool(name="store", bufs=8))
-        psum_acc = stack.enter_context(tc.psum_pool(name="psum_acc", bufs=4))
-        psum_m = stack.enter_context(tc.psum_pool(name="psum_m", bufs=2))
+        psum_acc = stack.enter_context(tc.psum_pool(name="psum_acc", bufs=6))
         psum_tp = stack.enter_context(tc.psum_pool(name="psum_tp", bufs=2))
 
         ident_bf = const.tile([P, P], BF16, name="ident_bf")
@@ -340,10 +339,7 @@ def tile_nonlocalblock_pa_kernel(
         def m_tile(b, ih, ob):
             cols = slice(ih * BANK, (ih + 1) * BANK)
             o_cols = slice(ob * P, (ob + 1) * P)
-            if b + 1 < B:
-                m_acc = psum_m.tile([P, BANK], F32, name="m_acc")
-            else:
-                m_acc = psum_acc.tile([P, BANK], F32, name="m_acc", tag="acc")
+            m_acc = psum_acc.tile([P, BANK], F32, name="m_acc", tag="acc")
             tp_tiles["m", b, ih, ob] = m_acc
             nc.tensor.matmul_mx(
                 out=m_acc[:],
@@ -359,13 +355,15 @@ def tile_nonlocalblock_pa_kernel(
             cols = slice(ih * BANK, (ih + 1) * BANK)
             o_cols = slice(ob * P, (ob + 1) * P)
             o_sb = store.tile([P, BANK], F32, name="o_sb")
-            nc.vector.tensor_tensor(out=o_sb[:], in0=tp_tiles["m", b, ih, ob][:], in1=x_sb[b][ob // 2][:, ob % 2, cols], op=ADD)
+            x_cols = x_sb[b][ob // 2][:, ob % 2, cols]
+            nc.vector.tensor_tensor(out=o_sb[:], in0=tp_tiles["m", b, ih, ob][:], in1=x_cols, op=ADD)
             nc.sync.dma_start(out=out_rows[b, o_cols, cols], in_=o_sb[:])
+        G_SLOT = (4, 8)
 
         def background_tensor(n):
-            b, k = divmod(n - 4, PACK)
-            if 0 <= b < B:
-                g_tile(b, k)
+            for b in range(B):
+                if 0 <= n - G_SLOT[b] < PACK:
+                    g_tile(b, n - G_SLOT[b])
             if 0 <= n - 5 < O_BLOCKS // 2:
                 w_tile(n - 5)
             b, k = divmod(n - 10, J_BLOCKS)
@@ -378,9 +376,9 @@ def tile_nonlocalblock_pa_kernel(
                     m_tile(b, tile_no // O_BLOCKS, tile_no % O_BLOCKS)
 
         def background_out(n):
-            b, k = divmod(n - 4, PACK)
-            if 0 <= b < B:
-                g_tile_out(b, k)
+            for b in range(B):
+                if 0 <= n - G_SLOT[b] < PACK:
+                    g_tile_out(b, n - G_SLOT[b])
             if 0 <= n - 5 < O_BLOCKS // 2:
                 w_tile_out(n - 5)
             b, k = divmod(n - 10, J_BLOCKS)
@@ -399,9 +397,9 @@ def tile_nonlocalblock_pa_kernel(
                     regroup(r, k)
                 if 1 <= k < 1 + I_HALVES:
                     quantise_attn(r, k - 1)
-            b, k = divmod(n - 4 - 4, PACK)
-            if 0 <= b < B and k < J_PASSES:
-                g_quantise(b, k)
+            for b in range(B):
+                if 0 <= n - G_SLOT[b] - 4 < J_PASSES:
+                    g_quantise(b, n - G_SLOT[b] - 4)
             if n - 5 == O_BLOCKS // 2 + 1:
                 nc.vector.quantize_mx(out=w_codes[:].bitcast(FP8X4), scales=w_scales[:], in_=w_grouped[:])
             b, k = divmod(n - 10 - 3, J_BLOCKS)

@@ -10,7 +10,6 @@ U8 = mybir.dt.uint8
 FP8X4 = mybir.dt.float8_e4m3fn_x4
 ADD = mybir.AluOpType.add
 MAX = mybir.AluOpType.max
-MULT = mybir.AluOpType.mult
 EXP = mybir.ActivationFunctionType.Exp
 COPY = mybir.ActivationFunctionType.Copy
 X_AXIS = mybir.AxisListType.X
@@ -132,29 +131,26 @@ def tile_nonlocalblock_pa_kernel(
         for g in range(J_PASSES):
             load_phi(1, g)
 
-        pos_f32 = const.tile([P, J_BLOCKS, I_BLOCKS, P], F32, name="pos_f32")
-        for ih in range(I_HALVES):
-            blocks = slice(ih * BANK_BLOCKS, (ih + 1) * BANK_BLOCKS)
-            for t in range(PACK):
-                nc.vector.tensor_copy(out=pos_f32[:, t, blocks, :], in_=pos_sb[0][ih][:, :, t * P : (t + 1) * P])
-        for t in range(PACK):
-          for ih in range(I_HALVES):
-            nc.gpsimd.tensor_scalar(
-                out=pos_f32[:, PACK + t, ih * BANK_BLOCKS : (ih + 1) * BANK_BLOCKS, :],
-                in0=pos_sb[1][ih][:, :, t * P : (t + 1) * P],
-                scalar1=1.0,
-                scalar2=0.0,
-                op0=MULT,
-                op1=ADD,
-            )
+        pos_t = const.tile([P, J_BLOCKS, N], BF16, name="pos_t")
+        for jb in range(J_BLOCKS):
+            g, t = divmod(jb, PACK)
+            for ih in range(I_HALVES):
+                pt = psum_tp.tile([P, BANK_BLOCKS, P], BF16, name="pt", tag="tp")
+                for a in range(BANK_BLOCKS):
+                    nc.tensor.transpose(pt[:, a, :], pos_sb[g][ih][:, a, t * P : (t + 1) * P], ident_bf[:])
+                dst = pos_t[:, jb, ih * BANK : (ih + 1) * BANK]
+                if ih == 0:
+                    nc.vector.tensor_copy(out=dst, in_=pt[:].rearrange("p a i -> p (a i)"))
+                else:
+                    nc.scalar.copy(out=dst, in_=pt[:].rearrange("p a i -> p (a i)"))
         x_sb = [load_x(0)]
         for b in range(B):
             for t in range(PACK):
                 nc.gpsimd.tensor_tensor(out=gp_sb[b][:, t, :], in0=gp_sb[b][:, t, :], in1=ped_sb[:, t, :], op=ADD)
 
         acc = {}
-        bank_max = {}
-        bank_sum = {}
+        s_sb = {}
+        e_sum = {}
         e_sb = {}
         attn_bf = {}
         grouped = {}
@@ -176,17 +172,6 @@ def tile_nonlocalblock_pa_kernel(
         y_scales = {}
         tp_tiles = {}
 
-        def add_pos(m, a):
-            n, ih = divmod(m, I_HALVES)
-            nc.tensor.matmul(
-                out=acc[m][:, a * P : (a + 1) * P],
-                lhsT=pos_f32[:, n % J_BLOCKS, ih * BANK_BLOCKS + a, :],
-                rhs=ident_f32[:],
-                start=False,
-                stop=(a == BANK_BLOCKS - 1),
-                is_transpose=True,
-            )
-
         def scores(n):
             b, jb = divmod(n, J_BLOCKS)
             g, t = divmod(jb, PACK)
@@ -199,47 +184,32 @@ def tile_nonlocalblock_pa_kernel(
                         lhsT=phi_sb[b][g][:, k, t * P : (t + 1) * P],
                         rhs=theta_sb[b][ih][:, k, :],
                         start=(k == 0),
-                        stop=False,
+                        stop=(k == IC_CHUNKS - 1),
                     )
-            for ih in range(I_HALVES):
-                for a in range(BANK_BLOCKS):
-                    add_pos(n * I_HALVES + ih, a)
 
-        def bank_maximum(m):
+        def add_pos(m):
             n, ih = divmod(m, I_HALVES)
             if ih == 0:
-                bank_max[n] = stats.tile([P, I_HALVES], F32, name="bank_max")
-            nc.vector.tensor_reduce(out=bank_max[n][:, ih : ih + 1], in_=acc[m][:], axis=X_AXIS, op=MAX)
+                s_sb[n] = soft.tile([P, N], F32, name="s_sb", bufs=3)
+            cols = slice(ih * BANK, (ih + 1) * BANK)
+            nc.vector.tensor_tensor(out=s_sb[n][:, cols], in0=acc[m][:], in1=pos_t[:, n % J_BLOCKS, cols], op=ADD)
 
         def exponentials(n):
             neg_max = stats.tile([P, 1], F32, name="neg_max")
-            nc.vector.tensor_reduce(out=neg_max[:], in_=bank_max[n][:], axis=X_AXIS, op=MAX, negate=True)
             e_sb[n] = soft.tile([P, N], F32, name="e_sb", bufs=3)
-            bank_sum[n] = stats.tile([P, I_HALVES], F32, name="bank_sum")
-            for ih in range(I_HALVES):
-                nc.scalar.activation(
-                    out=e_sb[n][:, ih * BANK : (ih + 1) * BANK],
-                    in_=acc[n * I_HALVES + ih][:],
-                    func=EXP,
-                    bias=neg_max[:],
-                    scale=1.0,
-                    accum_out=bank_sum[n][:, ih : ih + 1],
-                )
+            e_sum[n] = stats.tile([P, 1], F32, name="e_sum")
+            nc.vector.tensor_reduce(out=neg_max[:], in_=s_sb[n][:], axis=X_AXIS, op=MAX, negate=True)
+            nc.scalar.activation(
+                out=e_sb[n][:], in_=s_sb[n][:], func=EXP, bias=neg_max[:], scale=1.0, accum_out=e_sum[n][:]
+            )
 
         def normalise(n):
             r, t = divmod(n, PACK)
             if t == 0:
                 attn_bf[r] = soft.tile([P, PACK, N], BF16, name="attn_bf")
-            e_sum = stats.tile([P, 1], F32, name="e_sum")
-            nc.vector.tensor_reduce(out=e_sum[:], in_=bank_sum[n][:], axis=X_AXIS, op=ADD)
             r_sum = stats.tile([P, 1], F32, name="r_sum")
-            nc.vector.reciprocal(out=r_sum[:], in_=e_sum[:])
-            if n % 2 == 1:
-                nc.vector.tensor_scalar(
-                    out=attn_bf[r][:, t, :], in0=e_sb[n][:], scalar1=r_sum[:], scalar2=None, op0=MULT
-                )
-            else:
-                nc.scalar.activation(out=attn_bf[r][:, t, :], in_=e_sb[n][:], func=COPY, scale=r_sum[:])
+            nc.vector.reciprocal(out=r_sum[:], in_=e_sum[n][:])
+            nc.scalar.activation(out=attn_bf[r][:, t, :], in_=e_sb[n][:], func=COPY, scale=r_sum[:])
 
         def regroup(r, ih):
             if ih == 0:
@@ -367,9 +337,9 @@ def tile_nonlocalblock_pa_kernel(
             if 0 <= n - 5 < O_BLOCKS // 2:
                 w_tile(n - 5)
             b, k = divmod(n - 10, J_BLOCKS)
-            if 0 <= b < B and k < 4:
-                y_chunk(b, 2 * k)
-                y_chunk(b, 2 * k + 1)
+            if 0 <= b < B and k < I_BLOCKS // 2:
+                for ic in range(2 * k, 2 * k + 2):
+                    y_chunk(b, ic)
             b, k = divmod(n - 14, J_BLOCKS)
             if 0 <= b < B and k < 16 // 2:
                 for tile_no in range(2 * k, 2 * k + 2):
@@ -382,9 +352,9 @@ def tile_nonlocalblock_pa_kernel(
             if 0 <= n - 5 < O_BLOCKS // 2:
                 w_tile_out(n - 5)
             b, k = divmod(n - 10, J_BLOCKS)
-            if 0 <= b < B and k < 4:
-                y_chunk_out(b, 2 * k)
-                y_chunk_out(b, 2 * k + 1)
+            if 0 <= b < B and k < I_BLOCKS // 2:
+                for ic in range(2 * k, 2 * k + 2):
+                    y_chunk_out(b, ic)
             b, k = divmod(n - 14, J_BLOCKS)
             if 0 <= b < B and k < 16 // 2:
                 for tile_no in range(2 * k, 2 * k + 2):
@@ -403,7 +373,7 @@ def tile_nonlocalblock_pa_kernel(
             if n - 5 == O_BLOCKS // 2 + 1:
                 nc.vector.quantize_mx(out=w_codes[:].bitcast(FP8X4), scales=w_scales[:], in_=w_grouped[:])
             b, k = divmod(n - 10 - 3, J_BLOCKS)
-            if 0 <= b < B and (k == 0 or k == 2):
+            if 0 <= b < B and k % 2 == 0 and k // 2 < I_HALVES:
                 y_quantise(b, k // 2)
 
         for n in range(34):
@@ -411,8 +381,8 @@ def tile_nonlocalblock_pa_kernel(
                 scores(n)
             background_out(n - 1)
             if n < SLOTS:
-                bank_maximum(2 * n)
-                bank_maximum(2 * n + 1)
+                add_pos(2 * n)
+                add_pos(2 * n + 1)
                 exponentials(n)
             if 1 <= n < SLOTS + 1:
                 normalise(n - 1)

@@ -9,6 +9,7 @@ U32 = mybir.dt.uint32
 U8 = mybir.dt.uint8
 FP8X4 = mybir.dt.float8_e4m3fn_x4
 ADD = mybir.AluOpType.add
+MULT = mybir.AluOpType.mult
 MAX = mybir.AluOpType.max
 EXP = mybir.ActivationFunctionType.Exp
 COPY = mybir.ActivationFunctionType.Copy
@@ -30,8 +31,18 @@ O_BLOCKS = C // P
 I_BLOCKS = N // P
 BANK_BLOCKS = BANK // P
 SLOTS = B * J_BLOCKS
-S_BANKS = SLOTS * I_HALVES
+TENSOR_POS = (0, 2, 4, 5, 7)
+VECTOR_POS = [jb for jb in range(J_BLOCKS) if jb not in TENSOR_POS]
 
+G_SLOT = (4, 8)
+W_SLOT = 6
+Y_SLOT = (11, 19)
+M_SLOT = (13, 21)
+M_RATE = 4
+YC_V = ()
+SG = [(b, ih, ob) for b in range(B) for ih in range(2) for ob in range(8) if (ob % 4 == 3 if b == 0 else ih == 1 and ob % 3 == 0)]
+QL = 6
+NV = 1
 FLOPS = 3 * 2 * B * N * N * IC
 
 
@@ -50,8 +61,8 @@ def tile_nonlocalblock_pa_kernel(
         codes = stack.enter_context(tc.tile_pool(name="codes", bufs=2))
         late = stack.enter_context(tc.tile_pool(name="late", bufs=1))
         store = stack.enter_context(tc.tile_pool(name="store", bufs=8))
-        psum_acc = stack.enter_context(tc.psum_pool(name="psum_acc", bufs=6))
-        psum_tp = stack.enter_context(tc.psum_pool(name="psum_tp", bufs=2))
+        psum_acc = stack.enter_context(tc.psum_pool(name="psum_acc", bufs=4))
+        psum_tp = stack.enter_context(tc.psum_pool(name="psum_tp", bufs=4))
 
         ident_bf = const.tile([P, P], BF16, name="ident_bf")
         make_identity(nc, ident_bf[:])
@@ -103,7 +114,7 @@ def tile_nonlocalblock_pa_kernel(
             quarters = []
             for q in range(4):
                 if b == 0:
-                    x_q = late.tile([P, O_BLOCKS // 4, N], BF16, name="x_q", tag="pos%d" % q)
+                    x_q = late.tile([P, O_BLOCKS // 4, N], BF16, name="x_q", tag="x%d" % q)
                 else:
                     x_q = inputs.tile([P, O_BLOCKS // 4, N], BF16, name="x_q", tag=("theta0", "theta1", "phi0", "phi1")[q])
                 rows = slice(q * (C // 4), (q + 1) * (C // 4))
@@ -113,8 +124,8 @@ def tile_nonlocalblock_pa_kernel(
 
         load_theta(0, 0)
         load_phi(0, 0)
-        load_pos(0, 0)
         load_theta(0, 1)
+        load_pos(0, 0)
         load_pos(0, 1)
         load_phi(0, 1)
         load_pos(1, 0)
@@ -131,26 +142,29 @@ def tile_nonlocalblock_pa_kernel(
         for g in range(J_PASSES):
             load_phi(1, g)
 
-        pos_t = const.tile([P, J_BLOCKS, N], BF16, name="pos_t")
-        for jb in range(J_BLOCKS):
-            g, t = divmod(jb, PACK)
-            for ih in range(I_HALVES):
-                pt = psum_tp.tile([P, BANK_BLOCKS, P], BF16, name="pt", tag="tp")
-                for a in range(BANK_BLOCKS):
-                    nc.tensor.transpose(pt[:, a, :], pos_sb[g][ih][:, a, t * P : (t + 1) * P], ident_bf[:])
-                dst = pos_t[:, jb, ih * BANK : (ih + 1) * BANK]
-                if ih == 0:
-                    nc.vector.tensor_copy(out=dst, in_=pt[:].rearrange("p a i -> p (a i)"))
-                else:
-                    nc.scalar.copy(out=dst, in_=pt[:].rearrange("p a i -> p (a i)"))
+        pos_t = const.tile([P, len(VECTOR_POS), N], BF16, name="pos_t")
+
+        tp_tiles = {}
+
+        def transpose_pos(v, ih):
+            g, t = divmod(VECTOR_POS[v], PACK)
+            pt = psum_tp.tile([P, BANK_BLOCKS, P], BF16, name="pt", tag="tp")
+            tp_tiles["pos", v, ih] = pt
+            for a in range(BANK_BLOCKS):
+                nc.tensor.transpose(pt[:, a, :], pos_sb[g][ih][:, a, t * P : (t + 1) * P], ident_bf[:])
+
+        def transpose_pos_out(v, ih):
+            nc.scalar.copy(
+                out=pos_t[:, v, ih * BANK : (ih + 1) * BANK],
+                in_=tp_tiles["pos", v, ih][:].rearrange("p a i -> p (a i)"),
+            )
+
         x_sb = [load_x(0)]
-        for b in range(B):
-            for t in range(PACK):
-                nc.gpsimd.tensor_tensor(out=gp_sb[b][:, t, :], in0=gp_sb[b][:, t, :], in1=ped_sb[:, t, :], op=ADD)
 
         acc = {}
         s_sb = {}
         e_sum = {}
+        half_sums = {}
         e_sb = {}
         attn_bf = {}
         grouped = {}
@@ -170,34 +184,64 @@ def tile_nonlocalblock_pa_kernel(
         y_grouped = {}
         y_codes = {}
         y_scales = {}
-        tp_tiles = {}
 
-        def scores(n):
+        def scores(n, ih):
             b, jb = divmod(n, J_BLOCKS)
             g, t = divmod(jb, PACK)
-            for ih in range(I_HALVES):
-                m = n * I_HALVES + ih
-                acc[m] = psum_acc.tile([P, BANK], F32, name="acc")
-                for k in range(IC_CHUNKS):
+            on_tensor = jb in TENSOR_POS
+            m = n * I_HALVES + ih
+            acc[m] = psum_acc.tile([P, BANK], F32, name="acc")
+            for k in range(IC_CHUNKS):
+                nc.tensor.matmul(
+                    out=acc[m][:],
+                    lhsT=phi_sb[b][g][:, k, t * P : (t + 1) * P],
+                    rhs=theta_sb[b][ih][:, k, :],
+                    start=(k == 0),
+                    stop=(k == IC_CHUNKS - 1 and not on_tensor),
+                )
+            if on_tensor:
+                for a in range(BANK_BLOCKS):
                     nc.tensor.matmul(
-                        out=acc[m][:],
-                        lhsT=phi_sb[b][g][:, k, t * P : (t + 1) * P],
-                        rhs=theta_sb[b][ih][:, k, :],
-                        start=(k == 0),
-                        stop=(k == IC_CHUNKS - 1),
+                        out=acc[m][:, a * P : (a + 1) * P],
+                        lhsT=pos_sb[g][ih][:, a, t * P : (t + 1) * P],
+                        rhs=ident_bf[:],
+                        start=False,
+                        stop=(a == BANK_BLOCKS - 1),
                     )
 
         def add_pos(m):
             n, ih = divmod(m, I_HALVES)
             if ih == 0:
-                s_sb[n] = soft.tile([P, N], F32, name="s_sb", bufs=3)
+                s_sb[n] = soft.tile([P, N], F32, name="s_sb")
             cols = slice(ih * BANK, (ih + 1) * BANK)
-            nc.vector.tensor_tensor(out=s_sb[n][:, cols], in0=acc[m][:], in1=pos_t[:, n % J_BLOCKS, cols], op=ADD)
+            nc.vector.tensor_tensor(out=s_sb[n][:, cols], in0=acc[m][:], in1=pos_t[:, VECTOR_POS.index(n % J_BLOCKS), cols], op=ADD)
 
         def exponentials(n):
+            if n % J_BLOCKS in VECTOR_POS:
+                add_pos(2 * n)
+                add_pos(2 * n + 1)
             neg_max = stats.tile([P, 1], F32, name="neg_max")
             e_sb[n] = soft.tile([P, N], F32, name="e_sb", bufs=3)
             e_sum[n] = stats.tile([P, 1], F32, name="e_sum")
+            if n % J_BLOCKS in TENSOR_POS:
+                half_max = stats.tile([P, I_HALVES], F32, name="half_max")
+                half_sum = stats.tile([P, I_HALVES], F32, name="half_sum")
+                for ih in range(I_HALVES):
+                    nc.vector.tensor_reduce(
+                        out=half_max[:, ih : ih + 1], in_=acc[n * I_HALVES + ih][:], axis=X_AXIS, op=MAX
+                    )
+                nc.vector.tensor_reduce(out=neg_max[:], in_=half_max[:], axis=X_AXIS, op=MAX, negate=True)
+                for ih in range(I_HALVES):
+                    nc.scalar.activation(
+                        out=e_sb[n][:, ih * BANK : (ih + 1) * BANK],
+                        in_=acc[n * I_HALVES + ih][:],
+                        func=EXP,
+                        bias=neg_max[:],
+                        scale=1.0,
+                        accum_out=half_sum[:, ih : ih + 1],
+                    )
+                half_sums[n] = half_sum
+                return
             nc.vector.tensor_reduce(out=neg_max[:], in_=s_sb[n][:], axis=X_AXIS, op=MAX, negate=True)
             nc.scalar.activation(
                 out=e_sb[n][:], in_=s_sb[n][:], func=EXP, bias=neg_max[:], scale=1.0, accum_out=e_sum[n][:]
@@ -208,17 +252,24 @@ def tile_nonlocalblock_pa_kernel(
             if t == 0:
                 attn_bf[r] = soft.tile([P, PACK, N], BF16, name="attn_bf")
             r_sum = stats.tile([P, 1], F32, name="r_sum")
+            if n in half_sums:
+                nc.vector.tensor_reduce(out=e_sum[n][:], in_=half_sums[n][:], axis=X_AXIS, op=ADD)
             nc.vector.reciprocal(out=r_sum[:], in_=e_sum[n][:])
-            nc.scalar.activation(out=attn_bf[r][:, t, :], in_=e_sb[n][:], func=COPY, scale=r_sum[:])
+            if n == SLOTS - 1 and NV:
+                nc.vector.tensor_scalar(out=attn_bf[r][:, t, :], in0=e_sb[n][:], scalar1=r_sum[:], scalar2=None, op0=MULT)
+            else:
+                nc.scalar.activation(out=attn_bf[r][:, t, :], in_=e_sb[n][:], func=COPY, scale=r_sum[:])
 
-        def regroup(r, ih):
-            if ih == 0:
+        def regroup(r, q):
+            if q == 0:
                 grouped[r] = soft.tile([P, N, PACK], BF16, name="grouped", align_bytes=64)
-            cols = slice(ih * BANK, (ih + 1) * BANK)
-            nc.vector.tensor_copy(
-                out=grouped[r][:, cols, :].rearrange("p (c i) t -> p c t i", i=4),
-                in_=attn_bf[r][:, :, cols].rearrange("p t (c i) -> p c t i", i=4),
-            )
+            cols = slice(q * BANK // 2, (q + 1) * BANK // 2)
+            dst = grouped[r][:, cols, :].rearrange("p (c i) t -> p c t i", i=4)
+            src = attn_bf[r][:, :, cols].rearrange("p t (c i) -> p c t i", i=4)
+            if r == 3 and q % 4 == 3:
+                nc.scalar.copy(out=dst, in_=src)
+            else:
+                nc.vector.tensor_copy(out=dst, in_=src)
 
         def quantise_attn(r, ih):
             b, g = divmod(r, J_PASSES)
@@ -228,6 +279,9 @@ def tile_nonlocalblock_pa_kernel(
                 scales=attn_scales[b][:, g, cols],
                 in_=grouped[r][:, cols, :].rearrange("p i t -> p (i t)"),
             )
+
+        def g_add(b, t):
+            nc.vector.tensor_tensor(out=gp_sb[b][:, t, :], in0=gp_sb[b][:, t, :], in1=ped_sb[:, t, :], op=ADD)
 
         def g_tile(b, k):
             half, g = divmod(k, J_PASSES)
@@ -271,6 +325,9 @@ def tile_nonlocalblock_pa_kernel(
                 out=words[:, 2 * k * P : (2 * k + 2) * P, :], in_=tp_tiles["w", k][:].rearrange("p u o -> p o u")
             )
 
+        def w_quantise():
+            nc.vector.quantize_mx(out=w_codes[:].bitcast(FP8X4), scales=w_scales[:], in_=w_grouped[:])
+
         def y_chunk(b, ic):
             if ic == 0:
                 y_grouped[b] = late.tile([P, N, PACK], BF16, name="y_grouped", align_bytes=64)
@@ -291,9 +348,12 @@ def tile_nonlocalblock_pa_kernel(
                     )
 
         def y_chunk_out(b, ic):
-            nc.scalar.copy(
-                out=y_grouped[b][:, ic * P : (ic + 1) * P, :], in_=tp_tiles["y", b, ic][:].rearrange("p t i -> p i t")
-            )
+            dst = y_grouped[b][:, ic * P : (ic + 1) * P, :]
+            src = tp_tiles["y", b, ic][:].rearrange("p t i -> p i t")
+            if b == 1 and ic in YC_V:
+                nc.vector.tensor_copy(out=dst, in_=src)
+            else:
+                nc.scalar.copy(out=dst, in_=src)
 
         def y_quantise(b, ih):
             if ih == 0:
@@ -309,7 +369,10 @@ def tile_nonlocalblock_pa_kernel(
         def m_tile(b, ih, ob):
             cols = slice(ih * BANK, (ih + 1) * BANK)
             o_cols = slice(ob * P, (ob + 1) * P)
-            m_acc = psum_acc.tile([P, BANK], F32, name="m_acc", tag="acc")
+            if b == 1 and ob % 2 == 0:
+                m_acc = psum_acc.tile([P, BANK], F32, name="m_acc", tag="acc")
+            else:
+                m_acc = psum_tp.tile([P, BANK], F32, name="m_acc", tag="tp")
             tp_tiles["m", b, ih, ob] = m_acc
             nc.tensor.matmul_mx(
                 out=m_acc[:],
@@ -326,67 +389,71 @@ def tile_nonlocalblock_pa_kernel(
             o_cols = slice(ob * P, (ob + 1) * P)
             o_sb = store.tile([P, BANK], F32, name="o_sb")
             x_cols = x_sb[b][ob // 2][:, ob % 2, cols]
-            nc.vector.tensor_tensor(out=o_sb[:], in0=tp_tiles["m", b, ih, ob][:], in1=x_cols, op=ADD)
+            if (b, ih, ob) in SG:
+                nc.scalar.copy(out=o_sb[:], in_=tp_tiles["m", b, ih, ob][:])
+                nc.gpsimd.tensor_tensor(out=o_sb[:], in0=o_sb[:], in1=x_cols, op=ADD)
+            else:
+                nc.vector.tensor_tensor(out=o_sb[:], in0=tp_tiles["m", b, ih, ob][:], in1=x_cols, op=ADD)
             nc.sync.dma_start(out=out_rows[b, o_cols, cols], in_=o_sb[:])
-        G_SLOT = (4, 8)
 
-        def background_tensor(n):
-            for b in range(B):
-                if 0 <= n - G_SLOT[b] < PACK:
-                    g_tile(b, n - G_SLOT[b])
-            if 0 <= n - 5 < O_BLOCKS // 2:
-                w_tile(n - 5)
-            b, k = divmod(n - 10, J_BLOCKS)
-            if 0 <= b < B and k < I_BLOCKS // 2:
-                for ic in range(2 * k, 2 * k + 2):
-                    y_chunk(b, ic)
-            b, k = divmod(n - 14, J_BLOCKS)
-            if 0 <= b < B and k < 16 // 2:
-                for tile_no in range(2 * k, 2 * k + 2):
-                    m_tile(b, tile_no // O_BLOCKS, tile_no % O_BLOCKS)
+        tensor_jobs = {}
+        out_jobs = {}
+        vector_jobs = {}
 
-        def background_out(n):
-            for b in range(B):
-                if 0 <= n - G_SLOT[b] < PACK:
-                    g_tile_out(b, n - G_SLOT[b])
-            if 0 <= n - 5 < O_BLOCKS // 2:
-                w_tile_out(n - 5)
-            b, k = divmod(n - 10, J_BLOCKS)
-            if 0 <= b < B and k < I_BLOCKS // 2:
-                for ic in range(2 * k, 2 * k + 2):
-                    y_chunk_out(b, ic)
-            b, k = divmod(n - 14, J_BLOCKS)
-            if 0 <= b < B and k < 16 // 2:
-                for tile_no in range(2 * k, 2 * k + 2):
-                    m_tile_out(b, tile_no // O_BLOCKS, tile_no % O_BLOCKS)
+        def put(table, slot, job, *args):
+            table.setdefault(slot, []).append((job, args))
 
-        def background_quantise(n):
-            r, k = divmod(n - 4, PACK)
-            if 0 <= r < B * J_PASSES:
-                if k < I_HALVES:
-                    regroup(r, k)
-                if 1 <= k < 1 + I_HALVES:
-                    quantise_attn(r, k - 1)
-            for b in range(B):
-                if 0 <= n - G_SLOT[b] - 4 < J_PASSES:
-                    g_quantise(b, n - G_SLOT[b] - 4)
-            if n - 5 == O_BLOCKS // 2 + 1:
-                nc.vector.quantize_mx(out=w_codes[:].bitcast(FP8X4), scales=w_scales[:], in_=w_grouped[:])
-            b, k = divmod(n - 10 - 3, J_BLOCKS)
-            if 0 <= b < B and k % 2 == 0 and k // 2 < I_HALVES:
-                y_quantise(b, k // 2)
+        def run(jobs):
+            for job, args in jobs:
+                job(*args)
 
-        for n in range(34):
-            if n < SLOTS:
-                scores(n)
-            background_out(n - 1)
-            if n < SLOTS:
-                add_pos(2 * n)
-                add_pos(2 * n + 1)
-                exponentials(n)
-            if 1 <= n < SLOTS + 1:
-                normalise(n - 1)
-            background_quantise(n)
-            background_tensor(n)
-            if n == 10:
-                x_sb.append(load_x(1))
+        for v in range(len(VECTOR_POS)):
+            for ih in range(I_HALVES):
+                put(tensor_jobs, VECTOR_POS[v], transpose_pos, v, ih)
+                put(out_jobs, VECTOR_POS[v] + 1, transpose_pos_out, v, ih)
+        for b in range(B):
+            for t in range(PACK):
+                put(vector_jobs, G_SLOT[b] - 1, g_add, b, t)
+            for k in range(PACK):
+                put(tensor_jobs, G_SLOT[b] + k, g_tile, b, k)
+                put(out_jobs, G_SLOT[b] + k + 1, g_tile_out, b, k)
+            for g in range(J_PASSES):
+                put(vector_jobs, G_SLOT[b] + 4 + g, g_quantise, b, g)
+        for k in range(O_BLOCKS // 2):
+            put(tensor_jobs, W_SLOT + k, w_tile, k)
+            put(out_jobs, W_SLOT + k + 1, w_tile_out, k)
+        put(vector_jobs, W_SLOT + 5, w_quantise)
+        for r in range(B * J_PASSES):
+            for ih in range(I_HALVES):
+                put(vector_jobs, 4 * r + 5, regroup, r, 2 * ih)
+                put(vector_jobs, 4 * r + 5, regroup, r, 2 * ih + 1)
+                put(vector_jobs, 4 * r + QL, quantise_attn, r, ih)
+        for b in range(B):
+            for ic in range(I_BLOCKS):
+                put(tensor_jobs, Y_SLOT[b] + ic // 4, y_chunk, b, ic)
+                put(out_jobs, Y_SLOT[b] + ic // 4 + 1, y_chunk_out, b, ic)
+            for ih in range(I_HALVES):
+                put(vector_jobs, Y_SLOT[b] + ih + 1, y_quantise, b, ih)
+            for tile_no in range(16):
+                slot = M_SLOT[b] + tile_no // M_RATE
+                put(tensor_jobs, slot, m_tile, b, tile_no // O_BLOCKS, tile_no % O_BLOCKS)
+                put(out_jobs, slot + 1, m_tile_out, b, tile_no // O_BLOCKS, tile_no % O_BLOCKS)
+
+        if True:
+            for n in range(SLOTS + 14):
+                run(out_jobs.get(n, []))
+                jobs = tensor_jobs.get(n, [])
+                if n < SLOTS:
+                    scores(n, 0)
+                    run(jobs[: len(jobs) // 2])
+                    scores(n, 1)
+                    run(jobs[len(jobs) // 2 :])
+                else:
+                    run(jobs)
+                if 2 <= n < SLOTS + 2:
+                    normalise(n - 2)
+                if 1 <= n < SLOTS + 1:
+                    exponentials(n - 1)
+                run(vector_jobs.get(n, []))
+                if n == 10:
+                    x_sb.append(load_x(1))

@@ -13,6 +13,7 @@ MULT = mybir.AluOpType.mult
 MAX = mybir.AluOpType.max
 EXP = mybir.ActivationFunctionType.Exp
 COPY = mybir.ActivationFunctionType.Copy
+IDENT = mybir.ActivationFunctionType.Identity
 X_AXIS = mybir.AxisListType.X
 
 B = 2
@@ -31,18 +32,15 @@ O_BLOCKS = C // P
 I_BLOCKS = N // P
 BANK_BLOCKS = BANK // P
 SLOTS = B * J_BLOCKS
-TENSOR_POS = (0, 2, 4, 5, 7)
-VECTOR_POS = [jb for jb in range(J_BLOCKS) if jb not in TENSOR_POS]
+TENSOR_POS = (0, 5, 6, 7, 8, 9, 10, 13, 14, 15)
+VECTOR_POS = [n for n in range(SLOTS) if n not in TENSOR_POS]
+POS_T = [jb for jb in range(J_BLOCKS) if jb in VECTOR_POS or jb + J_BLOCKS in VECTOR_POS]
 
-G_SLOT = (4, 8)
-W_SLOT = 6
-Y_SLOT = (11, 19)
-M_SLOT = (13, 21)
-M_RATE = 4
-YC_V = ()
-SG = [(b, ih, ob) for b in range(B) for ih in range(2) for ob in range(8) if (ob % 4 == 3 if b == 0 else ih == 1 and ob % 3 == 0)]
-QL = 6
-NV = 1
+G_ADD = (5, 10)
+G_SLOT = (6, 12)
+W_SLOT = 8
+Y_SLOT = 12
+RG = 6
 FLOPS = 3 * 2 * B * N * N * IC
 
 
@@ -57,7 +55,7 @@ def tile_nonlocalblock_pa_kernel(
         const = stack.enter_context(tc.tile_pool(name="const", bufs=1))
         inputs = stack.enter_context(tc.tile_pool(name="inputs", bufs=2))
         soft = stack.enter_context(tc.tile_pool(name="soft", bufs=2))
-        stats = stack.enter_context(tc.tile_pool(name="stats", bufs=6))
+        stats = stack.enter_context(tc.tile_pool(name="stats", bufs=8))
         codes = stack.enter_context(tc.tile_pool(name="codes", bufs=2))
         late = stack.enter_context(tc.tile_pool(name="late", bufs=1))
         store = stack.enter_context(tc.tile_pool(name="store", bufs=8))
@@ -124,8 +122,8 @@ def tile_nonlocalblock_pa_kernel(
 
         load_theta(0, 0)
         load_phi(0, 0)
-        load_theta(0, 1)
         load_pos(0, 0)
+        load_theta(0, 1)
         load_pos(0, 1)
         load_phi(0, 1)
         load_pos(1, 0)
@@ -142,12 +140,12 @@ def tile_nonlocalblock_pa_kernel(
         for g in range(J_PASSES):
             load_phi(1, g)
 
-        pos_t = const.tile([P, len(VECTOR_POS), N], BF16, name="pos_t")
+        pos_t = const.tile([P, len(POS_T), N], BF16, name="pos_t")
 
         tp_tiles = {}
 
         def transpose_pos(v, ih):
-            g, t = divmod(VECTOR_POS[v], PACK)
+            g, t = divmod(POS_T[v], PACK)
             pt = psum_tp.tile([P, BANK_BLOCKS, P], BF16, name="pt", tag="tp")
             tp_tiles["pos", v, ih] = pt
             for a in range(BANK_BLOCKS):
@@ -164,7 +162,8 @@ def tile_nonlocalblock_pa_kernel(
         acc = {}
         s_sb = {}
         e_sum = {}
-        half_sums = {}
+        neg_max = {}
+        r_sum = {}
         e_sb = {}
         attn_bf = {}
         grouped = {}
@@ -188,7 +187,7 @@ def tile_nonlocalblock_pa_kernel(
         def scores(n, ih):
             b, jb = divmod(n, J_BLOCKS)
             g, t = divmod(jb, PACK)
-            on_tensor = jb in TENSOR_POS
+            on_tensor = n in TENSOR_POS
             m = n * I_HALVES + ih
             acc[m] = psum_acc.tile([P, BANK], F32, name="acc")
             for k in range(IC_CHUNKS):
@@ -214,62 +213,68 @@ def tile_nonlocalblock_pa_kernel(
             if ih == 0:
                 s_sb[n] = soft.tile([P, N], F32, name="s_sb")
             cols = slice(ih * BANK, (ih + 1) * BANK)
-            nc.vector.tensor_tensor(out=s_sb[n][:, cols], in0=acc[m][:], in1=pos_t[:, VECTOR_POS.index(n % J_BLOCKS), cols], op=ADD)
+            nc.vector.tensor_tensor(out=s_sb[n][:, cols], in0=acc[m][:], in1=pos_t[:, POS_T.index(n % J_BLOCKS), cols], op=ADD)
 
-        def exponentials(n):
-            if n % J_BLOCKS in VECTOR_POS:
+        def maximum(n):
+            if n in VECTOR_POS:
                 add_pos(2 * n)
                 add_pos(2 * n + 1)
-            neg_max = stats.tile([P, 1], F32, name="neg_max")
-            e_sb[n] = soft.tile([P, N], F32, name="e_sb", bufs=3)
-            e_sum[n] = stats.tile([P, 1], F32, name="e_sum")
-            if n % J_BLOCKS in TENSOR_POS:
+            neg_max[n] = stats.tile([P, 1], F32, name="neg_max_t")
+            if n in TENSOR_POS:
                 half_max = stats.tile([P, I_HALVES], F32, name="half_max")
-                half_sum = stats.tile([P, I_HALVES], F32, name="half_sum")
                 for ih in range(I_HALVES):
                     nc.vector.tensor_reduce(
                         out=half_max[:, ih : ih + 1], in_=acc[n * I_HALVES + ih][:], axis=X_AXIS, op=MAX
                     )
-                nc.vector.tensor_reduce(out=neg_max[:], in_=half_max[:], axis=X_AXIS, op=MAX, negate=True)
+                nc.vector.tensor_reduce(out=neg_max[n][:], in_=half_max[:], axis=X_AXIS, op=MAX, negate=True)
+            else:
+                nc.vector.tensor_reduce(out=neg_max[n][:], in_=s_sb[n][:], axis=X_AXIS, op=MAX, negate=True)
+
+        def exponentials(n):
+            e_sb[n] = soft.tile([P, N], F32, name="e_sb_t", bufs=4)
+            e_sum[n] = stats.tile([P, 1], F32, name="e_sum_t")
+            if n in TENSOR_POS:
+                half_sum = stats.tile([P, I_HALVES], F32, name="half_sum")
                 for ih in range(I_HALVES):
                     nc.scalar.activation(
                         out=e_sb[n][:, ih * BANK : (ih + 1) * BANK],
                         in_=acc[n * I_HALVES + ih][:],
                         func=EXP,
-                        bias=neg_max[:],
+                        bias=neg_max[n][:],
                         scale=1.0,
                         accum_out=half_sum[:, ih : ih + 1],
                     )
-                half_sums[n] = half_sum
-                return
-            nc.vector.tensor_reduce(out=neg_max[:], in_=s_sb[n][:], axis=X_AXIS, op=MAX, negate=True)
-            nc.scalar.activation(
-                out=e_sb[n][:], in_=s_sb[n][:], func=EXP, bias=neg_max[:], scale=1.0, accum_out=e_sum[n][:]
-            )
+                nc.scalar.activation(
+                    out=e_sum[n][:], in_=half_sum[:, 0:1], func=IDENT, bias=half_sum[:, 1:2], scale=1.0
+                )
+            else:
+                nc.scalar.activation(
+                    out=e_sb[n][:], in_=s_sb[n][:], func=EXP, bias=neg_max[n][:], scale=1.0, accum_out=e_sum[n][:]
+                )
+
+        def reciprocal_sum(n):
+            r_sum[n] = stats.tile([P, 1], F32, name="r_sum_t")
+            nc.vector.reciprocal(out=r_sum[n][:], in_=e_sum[n][:])
 
         def normalise(n):
             r, t = divmod(n, PACK)
             if t == 0:
-                attn_bf[r] = soft.tile([P, PACK, N], BF16, name="attn_bf")
-            r_sum = stats.tile([P, 1], F32, name="r_sum")
-            if n in half_sums:
-                nc.vector.tensor_reduce(out=e_sum[n][:], in_=half_sums[n][:], axis=X_AXIS, op=ADD)
-            nc.vector.reciprocal(out=r_sum[:], in_=e_sum[n][:])
-            if n == SLOTS - 1 and NV:
-                nc.vector.tensor_scalar(out=attn_bf[r][:, t, :], in0=e_sb[n][:], scalar1=r_sum[:], scalar2=None, op0=MULT)
+                attn_bf[r] = soft.tile([P, PACK, N], BF16, name="attn_bf_t")
+            if n >= SLOTS - 2:
+                nc.vector.tensor_scalar(
+                    out=attn_bf[r][:, t, :], in0=e_sb[n][:], scalar1=r_sum[n][:], scalar2=None, op0=MULT
+                )
             else:
-                nc.scalar.activation(out=attn_bf[r][:, t, :], in_=e_sb[n][:], func=COPY, scale=r_sum[:])
+                nc.scalar.activation(out=attn_bf[r][:, t, :], in_=e_sb[n][:], func=COPY, scale=r_sum[n][:])
 
-        def regroup(r, q):
-            if q == 0:
-                grouped[r] = soft.tile([P, N, PACK], BF16, name="grouped", align_bytes=64)
-            cols = slice(q * BANK // 2, (q + 1) * BANK // 2)
-            dst = grouped[r][:, cols, :].rearrange("p (c i) t -> p c t i", i=4)
-            src = attn_bf[r][:, :, cols].rearrange("p t (c i) -> p c t i", i=4)
-            if r == 3 and q % 4 == 3:
-                nc.scalar.copy(out=dst, in_=src)
-            else:
-                nc.vector.tensor_copy(out=dst, in_=src)
+        def regroup(r, first, last, engine_copy):
+            if first == 0:
+                grouped[r] = soft.tile([P, N, PACK], BF16, name="grouped_t", align_bytes=64)
+            cols = slice(first, last)
+            engine_copy(
+                out=grouped[r][:, cols, :].rearrange("p (c i) t -> p c t i", i=4),
+                in_=attn_bf[r][:, :, cols].rearrange("p t (c i) -> p c t i", i=4),
+            )
 
         def quantise_attn(r, ih):
             b, g = divmod(r, J_PASSES)
@@ -350,15 +355,12 @@ def tile_nonlocalblock_pa_kernel(
         def y_chunk_out(b, ic):
             dst = y_grouped[b][:, ic * P : (ic + 1) * P, :]
             src = tp_tiles["y", b, ic][:].rearrange("p t i -> p i t")
-            if b == 1 and ic in YC_V:
-                nc.vector.tensor_copy(out=dst, in_=src)
-            else:
-                nc.scalar.copy(out=dst, in_=src)
+            nc.scalar.copy(out=dst, in_=src)
 
         def y_quantise(b, ih):
             if ih == 0:
-                y_codes[b] = late.tile([P, N], U32, name="y_codes", align_bytes=64)
-                y_scales[b] = late.tile([P, N], U8, name="y_scales", align_bytes=64)
+                y_codes[b] = late.tile([P, N], U32, name="y_codes", bufs=2, align_bytes=64)
+                y_scales[b] = late.tile([P, N], U8, name="y_scales", bufs=2, align_bytes=64)
             cols = slice(ih * BANK, (ih + 1) * BANK)
             nc.vector.quantize_mx(
                 out=y_codes[b][:, cols].bitcast(FP8X4),
@@ -369,7 +371,7 @@ def tile_nonlocalblock_pa_kernel(
         def m_tile(b, ih, ob):
             cols = slice(ih * BANK, (ih + 1) * BANK)
             o_cols = slice(ob * P, (ob + 1) * P)
-            if b == 1 and ob % 2 == 0:
+            if b == 0 or ob % 2 == 0:
                 m_acc = psum_acc.tile([P, BANK], F32, name="m_acc", tag="acc")
             else:
                 m_acc = psum_tp.tile([P, BANK], F32, name="m_acc", tag="tp")
@@ -389,15 +391,11 @@ def tile_nonlocalblock_pa_kernel(
             o_cols = slice(ob * P, (ob + 1) * P)
             o_sb = store.tile([P, BANK], F32, name="o_sb")
             x_cols = x_sb[b][ob // 2][:, ob % 2, cols]
-            if (b, ih, ob) in SG:
-                nc.scalar.copy(out=o_sb[:], in_=tp_tiles["m", b, ih, ob][:])
-                nc.gpsimd.tensor_tensor(out=o_sb[:], in0=o_sb[:], in1=x_cols, op=ADD)
-            else:
-                nc.vector.tensor_tensor(out=o_sb[:], in0=tp_tiles["m", b, ih, ob][:], in1=x_cols, op=ADD)
+            nc.vector.tensor_tensor(out=o_sb[:], in0=tp_tiles["m", b, ih, ob][:], in1=x_cols, op=ADD)
             nc.sync.dma_start(out=out_rows[b, o_cols, cols], in_=o_sb[:])
 
         tensor_jobs = {}
-        out_jobs = {}
+        copy_jobs = {}
         vector_jobs = {}
 
         def put(table, slot, job, *args):
@@ -407,53 +405,107 @@ def tile_nonlocalblock_pa_kernel(
             for job, args in jobs:
                 job(*args)
 
-        for v in range(len(VECTOR_POS)):
+        for v in range(len(POS_T)):
             for ih in range(I_HALVES):
-                put(tensor_jobs, VECTOR_POS[v], transpose_pos, v, ih)
-                put(out_jobs, VECTOR_POS[v] + 1, transpose_pos_out, v, ih)
+                put(tensor_jobs, POS_T[v], transpose_pos, v, ih)
+                put(copy_jobs, POS_T[v] + 1, transpose_pos_out, v, ih)
         for b in range(B):
             for t in range(PACK):
-                put(vector_jobs, G_SLOT[b] - 1, g_add, b, t)
+                put(vector_jobs, G_ADD[b] + t // 2, g_add, b, t)
             for k in range(PACK):
-                put(tensor_jobs, G_SLOT[b] + k, g_tile, b, k)
-                put(out_jobs, G_SLOT[b] + k + 1, g_tile_out, b, k)
+                put(tensor_jobs, G_SLOT[b] + k // 2, g_tile, b, k)
+                put(copy_jobs, G_SLOT[b] + k // 2 + 1, g_tile_out, b, k)
             for g in range(J_PASSES):
-                put(vector_jobs, G_SLOT[b] + 4 + g, g_quantise, b, g)
+                put(vector_jobs, G_SLOT[b] + 3 + g, g_quantise, b, g)
         for k in range(O_BLOCKS // 2):
-            put(tensor_jobs, W_SLOT + k, w_tile, k)
-            put(out_jobs, W_SLOT + k + 1, w_tile_out, k)
-        put(vector_jobs, W_SLOT + 5, w_quantise)
-        for r in range(B * J_PASSES):
+            put(tensor_jobs, W_SLOT + k // 2, w_tile, k)
+            put(copy_jobs, W_SLOT + k // 2 + 1, w_tile_out, k)
+        put(vector_jobs, W_SLOT + 3, w_quantise)
+        for r in range(B * J_PASSES - 1):
             for ih in range(I_HALVES):
-                put(vector_jobs, 4 * r + 5, regroup, r, 2 * ih)
-                put(vector_jobs, 4 * r + 5, regroup, r, 2 * ih + 1)
-                put(vector_jobs, 4 * r + QL, quantise_attn, r, ih)
-        for b in range(B):
-            for ic in range(I_BLOCKS):
-                put(tensor_jobs, Y_SLOT[b] + ic // 4, y_chunk, b, ic)
-                put(out_jobs, Y_SLOT[b] + ic // 4 + 1, y_chunk_out, b, ic)
+                put(vector_jobs, 4 * r + RG + ih, regroup, r, ih * BANK, (ih + 1) * BANK, nc.vector.tensor_copy)
             for ih in range(I_HALVES):
-                put(vector_jobs, Y_SLOT[b] + ih + 1, y_quantise, b, ih)
-            for tile_no in range(16):
-                slot = M_SLOT[b] + tile_no // M_RATE
-                put(tensor_jobs, slot, m_tile, b, tile_no // O_BLOCKS, tile_no % O_BLOCKS)
-                put(out_jobs, slot + 1, m_tile_out, b, tile_no // O_BLOCKS, tile_no % O_BLOCKS)
+                put(vector_jobs, 4 * r + RG + 1, quantise_attn, r, ih)
+        for ic in range(I_BLOCKS):
+            put(tensor_jobs, Y_SLOT + ic // 2, y_chunk, 0, ic)
+            put(copy_jobs, Y_SLOT + ic // 2 + 1, y_chunk_out, 0, ic)
+        put(vector_jobs, Y_SLOT + 2, y_quantise, 0, 0)
 
-        if True:
-            for n in range(SLOTS + 14):
-                run(out_jobs.get(n, []))
-                jobs = tensor_jobs.get(n, [])
-                if n < SLOTS:
-                    scores(n, 0)
-                    run(jobs[: len(jobs) // 2])
-                    scores(n, 1)
-                    run(jobs[len(jobs) // 2 :])
-                else:
-                    run(jobs)
-                if 2 <= n < SLOTS + 2:
-                    normalise(n - 2)
-                if 1 <= n < SLOTS + 1:
-                    exponentials(n - 1)
-                run(vector_jobs.get(n, []))
-                if n == 10:
-                    x_sb.append(load_x(1))
+        def m0(first, last):
+            for i in range(first, last):
+                m_tile(0, i // O_BLOCKS, i % O_BLOCKS)
+
+        def m0_out(first, last):
+            for i in range(first, last):
+                m_tile_out(0, i // O_BLOCKS, i % O_BLOCKS)
+
+        put(tensor_jobs, SLOTS - 1, m0, 0, 2)
+
+        def slot(n):
+            jobs = tensor_jobs.get(n, [])
+            run(copy_jobs.get(n, []))
+            if 1 <= n:
+                maximum(n - 1)
+            if 2 <= n:
+                reciprocal_sum(n - 2)
+            if 3 <= n:
+                normalise(n - 3)
+            if 1 <= n:
+                exponentials(n - 1)
+            scores(n, 0)
+            run(jobs[: len(jobs) // 2])
+            scores(n, 1)
+            run(jobs[len(jobs) // 2 :])
+            run(vector_jobs.get(n, []))
+            if n == 8:
+                x_sb.append(load_x(1))
+
+        with ExitStack() as head:
+            head.enter_context(tc.manual_schedule(engines={mybir.EngineType.PE}))
+            slot(0)
+            slot(1)
+        with ExitStack():
+            for n in range(2, SLOTS):
+                slot(n)
+            last = SLOTS - 1
+            run(copy_jobs.get(SLOTS, []))
+            maximum(last)
+            normalise(last - 2)
+            exponentials(last)
+            run(vector_jobs.get(SLOTS, []))
+            reciprocal_sum(last - 1)
+            normalise(last - 1)
+            m0(2, 4)
+            m0_out(0, 2)
+            m0(4, 6)
+            y_quantise(0, 1)
+            m0_out(2, 3)
+            reciprocal_sum(last)
+            normalise(last)
+            r = B * J_PASSES - 1
+            regroup(r, 0, BANK, nc.vector.tensor_copy)
+            regroup(r, N - BANK // 2, N, nc.scalar.copy)
+            quantise_attn(r, 0)
+            regroup(r, BANK, N - BANK // 2, nc.vector.tensor_copy)
+            m0(6, 8)
+            m0_out(3, 4)
+            quantise_attn(r, 1)
+            for ic in range(4):
+                y_chunk(1, ic)
+                y_chunk_out(1, ic)
+            m0_out(4, 8)
+            m0(8, 12)
+            m0_out(8, 9)
+            y_quantise(1, 0)
+            for i in range(4):
+                y_chunk(1, 4 + i)
+                y_chunk_out(1, 4 + i)
+                m0_out(9 + i, 10 + i)
+                m0(12 + i, 13 + i)
+            m0_out(13, 15)
+            y_quantise(1, 1)
+            m0_out(15, 16)
+            for ih in range(I_HALVES):
+                for ob in range(O_BLOCKS):
+                    m_tile(1, ih, ob)
+                    m_tile_out(1, ih, ob)

@@ -13,7 +13,7 @@ MULT = mybir.AluOpType.mult
 MAX = mybir.AluOpType.max
 EXP = mybir.ActivationFunctionType.Exp
 COPY = mybir.ActivationFunctionType.Copy
-IDENT = mybir.ActivationFunctionType.Identity
+POW = mybir.AluOpType.pow
 X_AXIS = mybir.AxisListType.X
 
 B = 2
@@ -32,15 +32,17 @@ O_BLOCKS = C // P
 I_BLOCKS = N // P
 BANK_BLOCKS = BANK // P
 SLOTS = B * J_BLOCKS
-TENSOR_POS = (0, 5, 6, 7, 8, 9, 10, 13, 14, 15)
+TENSOR_POS = (0, 7, 8, 9, 10, 11, 12, 13, 14, 15)
 VECTOR_POS = [n for n in range(SLOTS) if n not in TENSOR_POS]
 POS_T = [jb for jb in range(J_BLOCKS) if jb in VECTOR_POS or jb + J_BLOCKS in VECTOR_POS]
 
-G_ADD = (5, 10)
-G_SLOT = (6, 12)
+G_ADD = (8, 10)
+G_SLOT = (10, 13)
+GQ = (13, 16)
 W_SLOT = 8
-Y_SLOT = 12
-RG = 6
+WQ = 12
+RG = 7
+E_BUFS = 7
 FLOPS = 3 * 2 * B * N * N * IC
 
 
@@ -58,14 +60,16 @@ def tile_nonlocalblock_pa_kernel(
         stats = stack.enter_context(tc.tile_pool(name="stats", bufs=8))
         codes = stack.enter_context(tc.tile_pool(name="codes", bufs=2))
         late = stack.enter_context(tc.tile_pool(name="late", bufs=1))
-        store = stack.enter_context(tc.tile_pool(name="store", bufs=8))
-        psum_acc = stack.enter_context(tc.psum_pool(name="psum_acc", bufs=4))
-        psum_tp = stack.enter_context(tc.psum_pool(name="psum_tp", bufs=4))
+        psum_acc = stack.enter_context(tc.psum_pool(name="psum_acc", bufs=6))
+        psum_tp = stack.enter_context(tc.psum_pool(name="psum_tp", bufs=2))
 
         ident_bf = const.tile([P, P], BF16, name="ident_bf")
         make_identity(nc, ident_bf[:])
         ident_f32 = const.tile([P, P], F32, name="ident_f32")
         make_identity(nc, ident_f32[:])
+
+        minus_one = const.tile([P, 1], F32, name="minus_one")
+        nc.gpsimd.memset(minus_one[:], -1.0)
 
         theta_sb = []
         phi_sb = []
@@ -163,6 +167,7 @@ def tile_nonlocalblock_pa_kernel(
         s_sb = {}
         e_sum = {}
         neg_max = {}
+        o_sb = {}
         r_sum = {}
         e_sb = {}
         attn_bf = {}
@@ -226,12 +231,19 @@ def tile_nonlocalblock_pa_kernel(
                     nc.vector.tensor_reduce(
                         out=half_max[:, ih : ih + 1], in_=acc[n * I_HALVES + ih][:], axis=X_AXIS, op=MAX
                     )
-                nc.vector.tensor_reduce(out=neg_max[n][:], in_=half_max[:], axis=X_AXIS, op=MAX, negate=True)
+                nc.gpsimd.tensor_scalar(
+                    out=neg_max[n][:],
+                    in0=half_max[:, 0:1],
+                    scalar1=half_max[:, 1:2],
+                    scalar2=-1.0,
+                    op0=MAX,
+                    op1=MULT,
+                )
             else:
                 nc.vector.tensor_reduce(out=neg_max[n][:], in_=s_sb[n][:], axis=X_AXIS, op=MAX, negate=True)
 
         def exponentials(n):
-            e_sb[n] = soft.tile([P, N], F32, name="e_sb_t", bufs=4)
+            e_sb[n] = soft.tile([P, N], F32, name="e_sb_t", bufs=E_BUFS)
             e_sum[n] = stats.tile([P, 1], F32, name="e_sum_t")
             if n in TENSOR_POS:
                 half_sum = stats.tile([P, I_HALVES], F32, name="half_sum")
@@ -244,9 +256,7 @@ def tile_nonlocalblock_pa_kernel(
                         scale=1.0,
                         accum_out=half_sum[:, ih : ih + 1],
                     )
-                nc.scalar.activation(
-                    out=e_sum[n][:], in_=half_sum[:, 0:1], func=IDENT, bias=half_sum[:, 1:2], scale=1.0
-                )
+                nc.gpsimd.tensor_tensor(out=e_sum[n][:], in0=half_sum[:, 0:1], in1=half_sum[:, 1:2], op=ADD)
             else:
                 nc.scalar.activation(
                     out=e_sb[n][:], in_=s_sb[n][:], func=EXP, bias=neg_max[n][:], scale=1.0, accum_out=e_sum[n][:]
@@ -254,7 +264,7 @@ def tile_nonlocalblock_pa_kernel(
 
         def reciprocal_sum(n):
             r_sum[n] = stats.tile([P, 1], F32, name="r_sum_t")
-            nc.vector.reciprocal(out=r_sum[n][:], in_=e_sum[n][:])
+            nc.gpsimd.tensor_tensor(out=r_sum[n][:], in0=e_sum[n][:], in1=minus_one[:], op=POW)
 
         def normalise(n):
             r, t = divmod(n, PACK)
@@ -276,17 +286,18 @@ def tile_nonlocalblock_pa_kernel(
                 in_=attn_bf[r][:, :, cols].rearrange("p t (c i) -> p c t i", i=4),
             )
 
-        def quantise_attn(r, ih):
+        def quantise_attn(r, first, last):
             b, g = divmod(r, J_PASSES)
-            cols = slice(ih * BANK, (ih + 1) * BANK)
+            cols = slice(first, last)
             nc.vector.quantize_mx(
                 out=attn_codes[b][:, g, cols].bitcast(FP8X4),
                 scales=attn_scales[b][:, g, cols],
                 in_=grouped[r][:, cols, :].rearrange("p i t -> p (i t)"),
             )
 
-        def g_add(b, t):
-            nc.vector.tensor_tensor(out=gp_sb[b][:, t, :], in0=gp_sb[b][:, t, :], in1=ped_sb[:, t, :], op=ADD)
+        def g_add(b, u):
+            rows = slice(2 * u, 2 * u + 2)
+            nc.vector.tensor_tensor(out=gp_sb[b][:, rows, :], in0=gp_sb[b][:, rows, :], in1=ped_sb[:, rows, :], op=ADD)
 
         def g_tile(b, k):
             half, g = divmod(k, J_PASSES)
@@ -306,11 +317,11 @@ def tile_nonlocalblock_pa_kernel(
                 in_=tp_tiles["g", b, k][:].rearrange("p a t c -> p a c t"),
             )
 
-        def g_quantise(b, g):
+        def g_quantise(b):
             nc.vector.quantize_mx(
-                out=g_codes[b][:, g, :].bitcast(FP8X4),
-                scales=g_scales[b][:, g, :],
-                in_=g_grouped[b][:, g, :, :].rearrange("p c t -> p (c t)"),
+                out=g_codes[b][:].rearrange("p g c -> p (g c)").bitcast(FP8X4),
+                scales=g_scales[b][:].rearrange("p g c -> p (g c)"),
+                in_=g_grouped[b][:].rearrange("p g c t -> p (g c t)"),
             )
 
         def w_tile(k):
@@ -371,10 +382,7 @@ def tile_nonlocalblock_pa_kernel(
         def m_tile(b, ih, ob):
             cols = slice(ih * BANK, (ih + 1) * BANK)
             o_cols = slice(ob * P, (ob + 1) * P)
-            if b == 0 or ob % 2 == 0:
-                m_acc = psum_acc.tile([P, BANK], F32, name="m_acc", tag="acc")
-            else:
-                m_acc = psum_tp.tile([P, BANK], F32, name="m_acc", tag="tp")
+            m_acc = psum_acc.tile([P, BANK], F32, name="m_acc", tag="acc")
             tp_tiles["m", b, ih, ob] = m_acc
             nc.tensor.matmul_mx(
                 out=m_acc[:],
@@ -386,13 +394,22 @@ def tile_nonlocalblock_pa_kernel(
                 stop=True,
             )
 
-        def m_tile_out(b, ih, ob):
+        def m_pair(b, ih, pair):
             cols = slice(ih * BANK, (ih + 1) * BANK)
-            o_cols = slice(ob * P, (ob + 1) * P)
-            o_sb = store.tile([P, BANK], F32, name="o_sb")
-            x_cols = x_sb[b][ob // 2][:, ob % 2, cols]
-            nc.vector.tensor_tensor(out=o_sb[:], in0=tp_tiles["m", b, ih, ob][:], in1=x_cols, op=ADD)
-            nc.sync.dma_start(out=out_rows[b, o_cols, cols], in_=o_sb[:])
+            o_tile = soft.tile([P, 2, BANK], F32, name="o_tile", tag="e_sb_t", bufs=E_BUFS)
+            o_sb[b, ih, pair] = o_tile
+            for a in range(2):
+                m_tile(b, ih, 2 * pair + a)
+                m_acc = tp_tiles["m", b, ih, 2 * pair + a]
+                x_cols = x_sb[b][pair][:, a, cols]
+                nc.vector.tensor_tensor(out=o_tile[:, a, :], in0=m_acc[:], in1=x_cols, op=ADD)
+
+        def m_store(b, ih, pair):
+            cols = slice(ih * BANK, (ih + 1) * BANK)
+            rows = slice(2 * pair * P, (2 * pair + 2) * P)
+            nc.sync.dma_start(
+                out=out_rows[b, rows, cols].rearrange("(a p) i -> p a i", p=P), in_=o_sb[b, ih, pair][:]
+            )
 
         tensor_jobs = {}
         copy_jobs = {}
@@ -407,39 +424,23 @@ def tile_nonlocalblock_pa_kernel(
 
         for v in range(len(POS_T)):
             for ih in range(I_HALVES):
-                put(tensor_jobs, POS_T[v], transpose_pos, v, ih)
-                put(copy_jobs, POS_T[v] + 1, transpose_pos_out, v, ih)
+                put(tensor_jobs, POS_T[v] - 1, transpose_pos, v, ih)
+                put(copy_jobs, POS_T[v], transpose_pos_out, v, ih)
         for b in range(B):
-            for t in range(PACK):
-                put(vector_jobs, G_ADD[b] + t // 2, g_add, b, t)
+            for u in range(2):
+                put(vector_jobs, G_ADD[b] + u, g_add, b, u)
             for k in range(PACK):
                 put(tensor_jobs, G_SLOT[b] + k // 2, g_tile, b, k)
                 put(copy_jobs, G_SLOT[b] + k // 2 + 1, g_tile_out, b, k)
-            for g in range(J_PASSES):
-                put(vector_jobs, G_SLOT[b] + 3 + g, g_quantise, b, g)
+            put(vector_jobs, GQ[b], g_quantise, b)
         for k in range(O_BLOCKS // 2):
             put(tensor_jobs, W_SLOT + k // 2, w_tile, k)
             put(copy_jobs, W_SLOT + k // 2 + 1, w_tile_out, k)
-        put(vector_jobs, W_SLOT + 3, w_quantise)
+        put(vector_jobs, WQ, w_quantise)
         for r in range(B * J_PASSES - 1):
             for ih in range(I_HALVES):
                 put(vector_jobs, 4 * r + RG + ih, regroup, r, ih * BANK, (ih + 1) * BANK, nc.vector.tensor_copy)
-            for ih in range(I_HALVES):
-                put(vector_jobs, 4 * r + RG + 1, quantise_attn, r, ih)
-        for ic in range(I_BLOCKS):
-            put(tensor_jobs, Y_SLOT + ic // 2, y_chunk, 0, ic)
-            put(copy_jobs, Y_SLOT + ic // 2 + 1, y_chunk_out, 0, ic)
-        put(vector_jobs, Y_SLOT + 2, y_quantise, 0, 0)
-
-        def m0(first, last):
-            for i in range(first, last):
-                m_tile(0, i // O_BLOCKS, i % O_BLOCKS)
-
-        def m0_out(first, last):
-            for i in range(first, last):
-                m_tile_out(0, i // O_BLOCKS, i % O_BLOCKS)
-
-        put(tensor_jobs, SLOTS - 1, m0, 0, 2)
+            put(vector_jobs, 4 * r + RG + 2, quantise_attn, r, 0, N)
 
         def slot(n):
             jobs = tensor_jobs.get(n, [])
@@ -460,52 +461,55 @@ def tile_nonlocalblock_pa_kernel(
             if n == 8:
                 x_sb.append(load_x(1))
 
-        with ExitStack() as head:
-            head.enter_context(tc.manual_schedule(engines={mybir.EngineType.PE}))
-            slot(0)
-            slot(1)
-        with ExitStack():
-            for n in range(2, SLOTS):
+        last = SLOTS - 1
+        r = B * J_PASSES - 1
+        half = BANK // 2
+
+        def y_chunks(b, first, end):
+            for ic in range(first, end):
+                y_chunk(b, ic)
+                y_chunk_out(b, ic)
+
+        def m_row(b, ih, pairs):
+            for pair in pairs:
+                m_pair(b, ih, pair)
+                m_store(b, ih, pair)
+
+        with tc.manual_schedule():
+            for n in range(SLOTS):
                 slot(n)
-            last = SLOTS - 1
             run(copy_jobs.get(SLOTS, []))
             maximum(last)
             normalise(last - 2)
+            y_chunks(0, 0, 1)
             exponentials(last)
             run(vector_jobs.get(SLOTS, []))
+            y_chunks(0, 1, 4)
             reciprocal_sum(last - 1)
             normalise(last - 1)
-            m0(2, 4)
-            m0_out(0, 2)
-            m0(4, 6)
-            y_quantise(0, 1)
-            m0_out(2, 3)
+            run(vector_jobs.get(SLOTS + 1, []))
             reciprocal_sum(last)
             normalise(last)
-            r = B * J_PASSES - 1
+            y_quantise(0, 0)
             regroup(r, 0, BANK, nc.vector.tensor_copy)
-            regroup(r, N - BANK // 2, N, nc.scalar.copy)
-            quantise_attn(r, 0)
-            regroup(r, BANK, N - BANK // 2, nc.vector.tensor_copy)
-            m0(6, 8)
-            m0_out(3, 4)
-            quantise_attn(r, 1)
-            for ic in range(4):
-                y_chunk(1, ic)
-                y_chunk_out(1, ic)
-            m0_out(4, 8)
-            m0(8, 12)
-            m0_out(8, 9)
+            y_chunks(0, 4, 8)
+            regroup(r, N - half, N, nc.scalar.copy)
+            m_row(0, 0, (0,))
+            quantise_attn(r, 0, BANK)
+            regroup(r, BANK, N - half, nc.vector.tensor_copy)
+            y_quantise(0, 1)
+            m_row(0, 0, (1,))
+            quantise_attn(r, BANK, N)
+            y_chunks(1, 0, 2)
+            m_row(0, 0, (2,))
+            y_chunks(1, 2, 4)
+            m_row(0, 0, (3,))
+            m_row(0, 1, (0,))
             y_quantise(1, 0)
-            for i in range(4):
-                y_chunk(1, 4 + i)
-                y_chunk_out(1, 4 + i)
-                m0_out(9 + i, 10 + i)
-                m0(12 + i, 13 + i)
-            m0_out(13, 15)
+            y_chunks(1, 4, 6)
+            m_row(0, 1, (1,))
+            y_chunks(1, 6, 8)
+            m_row(0, 1, (2,3))
             y_quantise(1, 1)
-            m0_out(15, 16)
-            for ih in range(I_HALVES):
-                for ob in range(O_BLOCKS):
-                    m_tile(1, ih, ob)
-                    m_tile_out(1, ih, ob)
+            m_row(1, 0, range(4))
+            m_row(1, 1, range(4))

@@ -13,7 +13,7 @@ MULT = mybir.AluOpType.mult
 MAX = mybir.AluOpType.max
 EXP = mybir.ActivationFunctionType.Exp
 COPY = mybir.ActivationFunctionType.Copy
-POW = mybir.AluOpType.pow
+IDENT = mybir.ActivationFunctionType.Identity
 X_AXIS = mybir.AxisListType.X
 
 B = 2
@@ -68,9 +68,6 @@ def tile_nonlocalblock_pa_kernel(
         ident_f32 = const.tile([P, P], F32, name="ident_f32")
         make_identity(nc, ident_f32[:])
 
-        minus_one = const.tile([P, 1], F32, name="minus_one")
-        nc.gpsimd.memset(minus_one[:], -1.0)
-
         theta_sb = []
         phi_sb = []
         gp_sb = []
@@ -124,8 +121,15 @@ def tile_nonlocalblock_pa_kernel(
                 quarters.append(x_q)
             return quarters
 
-        load_theta(0, 0)
-        load_phi(0, 0)
+        for k in range(0, IC_CHUNKS, 2):
+            ks = slice(k, k + 2)
+            rows = slice(k * P, (k + 2) * P)
+            nc.sync.dma_start(
+                out=theta_sb[0][0][:, ks, :], in_=theta[0, rows, 0:BANK].rearrange("(k p) i -> p k i", p=P)
+            )
+            nc.sync.dma_start(
+                out=phi_sb[0][0][:, ks, :], in_=phi[0, rows, 0:K_PASS].rearrange("(k p) j -> p k j", p=P)
+            )
         load_pos(0, 0)
         load_theta(0, 1)
         load_pos(0, 1)
@@ -231,14 +235,7 @@ def tile_nonlocalblock_pa_kernel(
                     nc.vector.tensor_reduce(
                         out=half_max[:, ih : ih + 1], in_=acc[n * I_HALVES + ih][:], axis=X_AXIS, op=MAX
                     )
-                nc.gpsimd.tensor_scalar(
-                    out=neg_max[n][:],
-                    in0=half_max[:, 0:1],
-                    scalar1=half_max[:, 1:2],
-                    scalar2=-1.0,
-                    op0=MAX,
-                    op1=MULT,
-                )
+                nc.vector.tensor_reduce(out=neg_max[n][:], in_=half_max[:], axis=X_AXIS, op=MAX, negate=True)
             else:
                 nc.vector.tensor_reduce(out=neg_max[n][:], in_=s_sb[n][:], axis=X_AXIS, op=MAX, negate=True)
 
@@ -256,7 +253,9 @@ def tile_nonlocalblock_pa_kernel(
                         scale=1.0,
                         accum_out=half_sum[:, ih : ih + 1],
                     )
-                nc.gpsimd.tensor_tensor(out=e_sum[n][:], in0=half_sum[:, 0:1], in1=half_sum[:, 1:2], op=ADD)
+                nc.scalar.activation(
+                    out=e_sum[n][:], in_=half_sum[:, 0:1], func=IDENT, bias=half_sum[:, 1:2], scale=1.0
+                )
             else:
                 nc.scalar.activation(
                     out=e_sb[n][:], in_=s_sb[n][:], func=EXP, bias=neg_max[n][:], scale=1.0, accum_out=e_sum[n][:]
@@ -264,7 +263,7 @@ def tile_nonlocalblock_pa_kernel(
 
         def reciprocal_sum(n):
             r_sum[n] = stats.tile([P, 1], F32, name="r_sum_t")
-            nc.gpsimd.tensor_tensor(out=r_sum[n][:], in0=e_sum[n][:], in1=minus_one[:], op=POW)
+            nc.vector.reciprocal(out=r_sum[n][:], in_=e_sum[n][:])
 
         def normalise(n):
             r, t = divmod(n, PACK)
@@ -348,7 +347,10 @@ def tile_nonlocalblock_pa_kernel(
             if ic == 0:
                 y_grouped[b] = late.tile([P, N, PACK], BF16, name="y_grouped", align_bytes=64)
             i_cols = slice(ic * P, (ic + 1) * P)
-            yt = psum_tp.tile([P, PACK, P], F32, name="yt", tag="tp")
+            if ic % 2 == 0:
+                yt = psum_tp.tile([P, PACK, P], F32, name="yt", tag="tp")
+            else:
+                yt = psum_acc.tile([P, PACK, P], F32, name="yt", tag="acc")
             tp_tiles["y", b, ic] = yt
             for t in range(PACK):
                 c_cols = slice(t * P, (t + 1) * P)
@@ -453,10 +455,20 @@ def tile_nonlocalblock_pa_kernel(
                 normalise(n - 3)
             if 1 <= n:
                 exponentials(n - 1)
-            scores(n, 0)
-            run(jobs[: len(jobs) // 2])
-            scores(n, 1)
-            run(jobs[len(jobs) // 2 :])
+            if n == 0:
+                scores(0, 0)
+                run(jobs[:1])
+                scores(1, 0)
+                scores(0, 1)
+                run(jobs[1:])
+            elif n == 1:
+                scores(1, 1)
+                run(jobs)
+            else:
+                scores(n, 0)
+                run(jobs[: len(jobs) // 2])
+                scores(n, 1)
+                run(jobs[len(jobs) // 2 :])
             run(vector_jobs.get(n, []))
             if n == 8:
                 x_sb.append(load_x(1))

@@ -32,17 +32,15 @@ O_BLOCKS = C // P
 I_BLOCKS = N // P
 BANK_BLOCKS = BANK // P
 SLOTS = B * J_BLOCKS
-TENSOR_POS = (0, 7, 8, 9, 10, 11, 12, 13, 14, 15)
-VECTOR_POS = [n for n in range(SLOTS) if n not in TENSOR_POS]
-POS_T = [jb for jb in range(J_BLOCKS) if jb in VECTOR_POS or jb + J_BLOCKS in VECTOR_POS]
+MATMUL_POS = 5
 
-G_ADD = (8, 10)
-G_SLOT = (10, 13)
-GQ = (13, 16)
-W_SLOT = 8
-WQ = 12
-RG = 7
-E_BUFS = 7
+G_ADD = (5, 8)
+G_SLOT = (10, 14)
+GQ = (14, 17)
+W_SLOT = 7
+WQ = 11
+RS = (7, 11, 14)
+E_BUFS = 8
 FLOPS = 3 * 2 * B * N * N * IC
 
 
@@ -148,27 +146,18 @@ def tile_nonlocalblock_pa_kernel(
         for g in range(J_PASSES):
             load_phi(1, g)
 
-        pos_t = const.tile([P, len(POS_T), N], BF16, name="pos_t")
-
-        tp_tiles = {}
-
-        def transpose_pos(v, ih):
-            g, t = divmod(POS_T[v], PACK)
-            pt = psum_tp.tile([P, BANK_BLOCKS, P], BF16, name="pt", tag="tp")
-            tp_tiles["pos", v, ih] = pt
-            for a in range(BANK_BLOCKS):
-                nc.tensor.transpose(pt[:, a, :], pos_sb[g][ih][:, a, t * P : (t + 1) * P], ident_bf[:])
-
-        def transpose_pos_out(v, ih):
-            nc.scalar.copy(
-                out=pos_t[:, v, ih * BANK : (ih + 1) * BANK],
-                in_=tp_tiles["pos", v, ih][:].rearrange("p a i -> p (a i)"),
+        first_col = (MATMUL_POS - PACK) * P
+        pos32 = []
+        for ih in range(I_HALVES):
+            pos32.append(const.tile([P, BANK_BLOCKS, K_PASS - first_col], F32, name="pos32_t", tag="pos32_%d" % ih))
+            nc.gpsimd.tensor_scalar(
+                out=pos32[ih][:], in0=pos_sb[1][ih][:, :, first_col:], scalar1=1.0, scalar2=0.0, op0=MULT, op1=ADD
             )
+        tp_tiles = {}
 
         x_sb = [load_x(0)]
 
         acc = {}
-        s_sb = {}
         e_sum = {}
         neg_max = {}
         o_sb = {}
@@ -196,7 +185,6 @@ def tile_nonlocalblock_pa_kernel(
         def scores(n, ih):
             b, jb = divmod(n, J_BLOCKS)
             g, t = divmod(jb, PACK)
-            on_tensor = n in TENSOR_POS
             m = n * I_HALVES + ih
             acc[m] = psum_acc.tile([P, BANK], F32, name="acc")
             for k in range(IC_CHUNKS):
@@ -205,10 +193,10 @@ def tile_nonlocalblock_pa_kernel(
                     lhsT=phi_sb[b][g][:, k, t * P : (t + 1) * P],
                     rhs=theta_sb[b][ih][:, k, :],
                     start=(k == 0),
-                    stop=(k == IC_CHUNKS - 1 and not on_tensor),
+                    stop=False,
                 )
-            if on_tensor:
-                for a in range(BANK_BLOCKS):
+            for a in range(BANK_BLOCKS):
+                if jb < MATMUL_POS:
                     nc.tensor.matmul(
                         out=acc[m][:, a * P : (a + 1) * P],
                         lhsT=pos_sb[g][ih][:, a, t * P : (t + 1) * P],
@@ -216,50 +204,41 @@ def tile_nonlocalblock_pa_kernel(
                         start=False,
                         stop=(a == BANK_BLOCKS - 1),
                     )
-
-        def add_pos(m):
-            n, ih = divmod(m, I_HALVES)
-            if ih == 0:
-                s_sb[n] = soft.tile([P, N], F32, name="s_sb")
-            cols = slice(ih * BANK, (ih + 1) * BANK)
-            nc.vector.tensor_tensor(out=s_sb[n][:, cols], in0=acc[m][:], in1=pos_t[:, POS_T.index(n % J_BLOCKS), cols], op=ADD)
+                else:
+                    nc.tensor.matmul(
+                        out=acc[m][:, a * P : (a + 1) * P],
+                        lhsT=pos32[ih][:, a, t * P - first_col : (t + 1) * P - first_col],
+                        rhs=ident_f32[:],
+                        is_transpose=True,
+                        start=False,
+                        stop=(a == BANK_BLOCKS - 1),
+                    )
 
         def maximum(n):
-            if n in VECTOR_POS:
-                add_pos(2 * n)
-                add_pos(2 * n + 1)
             neg_max[n] = stats.tile([P, 1], F32, name="neg_max_t")
-            if n in TENSOR_POS:
-                half_max = stats.tile([P, I_HALVES], F32, name="half_max")
-                for ih in range(I_HALVES):
-                    nc.vector.tensor_reduce(
-                        out=half_max[:, ih : ih + 1], in_=acc[n * I_HALVES + ih][:], axis=X_AXIS, op=MAX
-                    )
-                nc.vector.tensor_reduce(out=neg_max[n][:], in_=half_max[:], axis=X_AXIS, op=MAX, negate=True)
-            else:
-                nc.vector.tensor_reduce(out=neg_max[n][:], in_=s_sb[n][:], axis=X_AXIS, op=MAX, negate=True)
+            half_max = stats.tile([P, I_HALVES], F32, name="half_max")
+            for ih in range(I_HALVES):
+                nc.vector.tensor_reduce(
+                    out=half_max[:, ih : ih + 1], in_=acc[n * I_HALVES + ih][:], axis=X_AXIS, op=MAX
+                )
+            nc.vector.tensor_reduce(out=neg_max[n][:], in_=half_max[:], axis=X_AXIS, op=MAX, negate=True)
 
         def exponentials(n):
             e_sb[n] = soft.tile([P, N], F32, name="e_sb_t", bufs=E_BUFS)
             e_sum[n] = stats.tile([P, 1], F32, name="e_sum_t")
-            if n in TENSOR_POS:
-                half_sum = stats.tile([P, I_HALVES], F32, name="half_sum")
-                for ih in range(I_HALVES):
-                    nc.scalar.activation(
-                        out=e_sb[n][:, ih * BANK : (ih + 1) * BANK],
-                        in_=acc[n * I_HALVES + ih][:],
-                        func=EXP,
-                        bias=neg_max[n][:],
-                        scale=1.0,
-                        accum_out=half_sum[:, ih : ih + 1],
-                    )
+            half_sum = stats.tile([P, I_HALVES], F32, name="half_sum")
+            for ih in range(I_HALVES):
                 nc.scalar.activation(
-                    out=e_sum[n][:], in_=half_sum[:, 0:1], func=IDENT, bias=half_sum[:, 1:2], scale=1.0
+                    out=e_sb[n][:, ih * BANK : (ih + 1) * BANK],
+                    in_=acc[n * I_HALVES + ih][:],
+                    func=EXP,
+                    bias=neg_max[n][:],
+                    scale=1.0,
+                    accum_out=half_sum[:, ih : ih + 1],
                 )
-            else:
-                nc.scalar.activation(
-                    out=e_sb[n][:], in_=s_sb[n][:], func=EXP, bias=neg_max[n][:], scale=1.0, accum_out=e_sum[n][:]
-                )
+            nc.scalar.activation(
+                out=e_sum[n][:], in_=half_sum[:, 0:1], func=IDENT, bias=half_sum[:, 1:2], scale=1.0
+            )
 
         def reciprocal_sum(n):
             r_sum[n] = stats.tile([P, 1], F32, name="r_sum_t")
@@ -424,10 +403,6 @@ def tile_nonlocalblock_pa_kernel(
             for job, args in jobs:
                 job(*args)
 
-        for v in range(len(POS_T)):
-            for ih in range(I_HALVES):
-                put(tensor_jobs, POS_T[v] - 1, transpose_pos, v, ih)
-                put(copy_jobs, POS_T[v], transpose_pos_out, v, ih)
         for b in range(B):
             for u in range(2):
                 put(vector_jobs, G_ADD[b] + u, g_add, b, u)
@@ -441,8 +416,8 @@ def tile_nonlocalblock_pa_kernel(
         put(vector_jobs, WQ, w_quantise)
         for r in range(B * J_PASSES - 1):
             for ih in range(I_HALVES):
-                put(vector_jobs, 4 * r + RG + ih, regroup, r, ih * BANK, (ih + 1) * BANK, nc.vector.tensor_copy)
-            put(vector_jobs, 4 * r + RG + 2, quantise_attn, r, 0, N)
+                put(vector_jobs, RS[r] + ih, regroup, r, ih * BANK, (ih + 1) * BANK, nc.vector.tensor_copy)
+            put(vector_jobs, RS[r] + 2, quantise_attn, r, 0, N)
 
         def slot(n):
             jobs = tensor_jobs.get(n, [])
@@ -457,13 +432,10 @@ def tile_nonlocalblock_pa_kernel(
                 exponentials(n - 1)
             if n == 0:
                 scores(0, 0)
-                run(jobs[:1])
                 scores(1, 0)
                 scores(0, 1)
-                run(jobs[1:])
             elif n == 1:
                 scores(1, 1)
-                run(jobs)
             else:
                 scores(n, 0)
                 run(jobs[: len(jobs) // 2])
@@ -475,7 +447,6 @@ def tile_nonlocalblock_pa_kernel(
 
         last = SLOTS - 1
         r = B * J_PASSES - 1
-        half = BANK // 2
 
         def y_chunks(b, first, end):
             for ic in range(first, end):
@@ -505,10 +476,9 @@ def tile_nonlocalblock_pa_kernel(
             y_quantise(0, 0)
             regroup(r, 0, BANK, nc.vector.tensor_copy)
             y_chunks(0, 4, 8)
-            regroup(r, N - half, N, nc.scalar.copy)
+            regroup(r, BANK, N, nc.scalar.copy)
             m_row(0, 0, (0,))
             quantise_attn(r, 0, BANK)
-            regroup(r, BANK, N - half, nc.vector.tensor_copy)
             y_quantise(0, 1)
             m_row(0, 0, (1,))
             quantise_attn(r, BANK, N)

@@ -34,13 +34,13 @@ BANK_BLOCKS = BANK // P
 SLOTS = B * J_BLOCKS
 MATMUL_POS = 5
 
-G_ADD = (5, 8)
-G_SLOT = (10, 14)
-GQ = (14, 17)
-W_SLOT = 7
-WQ = 11
-RS = (7, 11, 14)
-E_BUFS = 8
+G_ADD = (4, 8)
+G_SLOT = (8, 12)
+GQ = (12, 16)
+W_SLOT = 6
+WQ = 10
+RS = (7, 12, 14)
+E_BUFS = 7
 FLOPS = 3 * 2 * B * N * N * IC
 
 
@@ -168,6 +168,7 @@ def tile_nonlocalblock_pa_kernel(
         attn_codes = []
         attn_scales = []
         g_grouped = {}
+        g_bf = {}
         g_codes = []
         g_scales = []
         for b in range(B):
@@ -273,26 +274,38 @@ def tile_nonlocalblock_pa_kernel(
                 in_=grouped[r][:, cols, :].rearrange("p i t -> p (i t)"),
             )
 
-        def g_add(b, u):
-            rows = slice(2 * u, 2 * u + 2)
-            nc.vector.tensor_tensor(out=gp_sb[b][:, rows, :], in0=gp_sb[b][:, rows, :], in1=ped_sb[:, rows, :], op=ADD)
+        def g_add(b, row):
+            if row == 0:
+                if b == 0:
+                    g_bf[b] = soft.tile([P, PACK, N], BF16, name="g_bf_t", bufs=1)
+                else:
+                    g_bf[b] = inputs.tile([P, PACK, N], BF16, name="g_bf_t", tag="gp")
+            pairs = "p (u e w) -> p u w e"
+            nc.vector.tensor_tensor(
+                out=g_bf[b][:, row, :].rearrange("p (u w e) -> p u w e", w=P, e=2),
+                in0=gp_sb[b][:, row, :].rearrange(pairs, e=2, w=P),
+                in1=ped_sb[:, row, :].rearrange(pairs, e=2, w=P),
+                op=ADD,
+            )
 
         def g_tile(b, k):
             half, g = divmod(k, J_PASSES)
             if k == 0:
-                g_grouped[b] = soft.tile([P, J_PASSES, IC, PACK], BF16, name="g_grouped", bufs=1, align_bytes=64)
-            pg = psum_tp.tile([P, 2, PACK, P], BF16, name="pg", tag="tp")
+                g_grouped[b] = soft.tile([P, J_PASSES, IC, PACK], BF16, name="g_grouped_t", bufs=1, align_bytes=64)
+            pg = psum_tp.tile([P, 2, 2, P], F32, name="pg", tag="tp")
             tp_tiles["g", b, k] = pg
             for a in range(2):
-                for t in range(PACK):
-                    jb = g * PACK + t
-                    nc.tensor.transpose(pg[:, a, t, :], gp_sb[b][:, 2 * half + a, jb * P : (jb + 1) * P], ident_bf[:])
+                words = g_bf[b][:, 2 * half + a, :].bitcast(F32)
+                for u in range(2):
+                    first = (2 * g + u) * P
+                    nc.tensor.transpose(pg[:, a, u, :], words[:, first : first + P], ident_f32[:])
 
         def g_tile_out(b, k):
             half, g = divmod(k, J_PASSES)
+            words = g_grouped[b][:].rearrange("p g c t -> p (g c t)").bitcast(F32).rearrange("p (g c u) -> p g c u", g=2, u=2)
             nc.scalar.copy(
-                out=g_grouped[b][:, g, 2 * half * P : (2 * half + 2) * P, :].rearrange("p (a c) t -> p a c t", a=2),
-                in_=tp_tiles["g", b, k][:].rearrange("p a t c -> p a c t"),
+                out=words[:, g, 2 * half * P : (2 * half + 2) * P, :].rearrange("p (a c) u -> p a c u", a=2),
+                in_=tp_tiles["g", b, k][:].rearrange("p a u c -> p a c u"),
             )
 
         def g_quantise(b):
@@ -404,8 +417,8 @@ def tile_nonlocalblock_pa_kernel(
                 job(*args)
 
         for b in range(B):
-            for u in range(2):
-                put(vector_jobs, G_ADD[b] + u, g_add, b, u)
+            for row in range(PACK):
+                put(vector_jobs, G_ADD[b] + row, g_add, b, row)
             for k in range(PACK):
                 put(tensor_jobs, G_SLOT[b] + k // 2, g_tile, b, k)
                 put(copy_jobs, G_SLOT[b] + k // 2 + 1, g_tile_out, b, k)

@@ -34,13 +34,14 @@ BANK_BLOCKS = BANK // P
 SLOTS = B * J_BLOCKS
 MATMUL_POS = 5
 
-G_ADD = (4, 8)
+G_ADD = (3, 7)
 G_SLOT = (8, 12)
 GQ = (12, 16)
 W_SLOT = 6
 WQ = 10
 RS = (7, 12, 14)
 E_BUFS = 7
+VECTOR_NORM = (8, 10, 14, 15)
 FLOPS = 3 * 2 * B * N * N * IC
 
 
@@ -101,10 +102,10 @@ def tile_nonlocalblock_pa_kernel(
                 in_=pos_embedding[0, rows, cols].rearrange("(a p) j -> p a j", p=P),
             )
 
-        def load_g(b):
+        def load_rows(tile, rows, u):
             nc.sync.dma_start(
-                out=gp_sb[b][:].rearrange("p (u e) j -> p u (e j)", u=2),
-                in_=g_proj[b].rearrange("(u p e) j -> p u (e j)", u=2, p=P),
+                out=tile[:, 2 * u : 2 * u + 2, :].rearrange("p e j -> p (e j)"),
+                in_=rows[u * 2 * P : (u + 1) * 2 * P, :].rearrange("(p e) j -> p (e j)", p=P),
             )
 
         def load_x(b):
@@ -134,17 +135,16 @@ def tile_nonlocalblock_pa_kernel(
         load_phi(0, 1)
         load_pos(1, 0)
         load_pos(1, 1)
-        nc.sync.dma_start(
-            out=ped_sb[:].rearrange("p (u e) j -> p u (e j)", u=2),
-            in_=pos_embedding_decoder[0].rearrange("(u p e) h w -> p u (e h w)", u=2, p=P),
-        )
-        load_g(0)
-        load_g(1)
+        for u in range(2):
+            load_rows(ped_sb, pos_embedding_decoder[0].rearrange("c h w -> c (h w)"), u)
+            load_rows(gp_sb[0], g_proj[0], u)
         nc.sync.dma_start(out=w_sb[:], in_=w_mask.rearrange("(a p) c -> p a c", p=P))
-        for ih in range(I_HALVES):
-            load_theta(1, ih)
-        for g in range(J_PASSES):
-            load_phi(1, g)
+        load_theta(1, 0)
+        load_phi(1, 0)
+        load_theta(1, 1)
+        for u in range(2):
+            load_rows(gp_sb[1], g_proj[1], u)
+        load_phi(1, 1)
 
         first_col = (MATMUL_POS - PACK) * P
         pos32 = []
@@ -160,6 +160,7 @@ def tile_nonlocalblock_pa_kernel(
         acc = {}
         e_sum = {}
         neg_max = {}
+        half_max = {}
         o_sb = {}
         r_sum = {}
         e_sb = {}
@@ -215,14 +216,16 @@ def tile_nonlocalblock_pa_kernel(
                         stop=(a == BANK_BLOCKS - 1),
                     )
 
+        def half_maximum(n, ih):
+            if ih == 0:
+                half_max[n] = stats.tile([P, I_HALVES], F32, name="half_max_t")
+            nc.vector.tensor_reduce(
+                out=half_max[n][:, ih : ih + 1], in_=acc[n * I_HALVES + ih][:], axis=X_AXIS, op=MAX
+            )
+
         def maximum(n):
             neg_max[n] = stats.tile([P, 1], F32, name="neg_max_t")
-            half_max = stats.tile([P, I_HALVES], F32, name="half_max")
-            for ih in range(I_HALVES):
-                nc.vector.tensor_reduce(
-                    out=half_max[:, ih : ih + 1], in_=acc[n * I_HALVES + ih][:], axis=X_AXIS, op=MAX
-                )
-            nc.vector.tensor_reduce(out=neg_max[n][:], in_=half_max[:], axis=X_AXIS, op=MAX, negate=True)
+            nc.vector.tensor_reduce(out=neg_max[n][:], in_=half_max[n][:], axis=X_AXIS, op=MAX, negate=True)
 
         def exponentials(n):
             e_sb[n] = soft.tile([P, N], F32, name="e_sb_t", bufs=E_BUFS)
@@ -249,7 +252,7 @@ def tile_nonlocalblock_pa_kernel(
             r, t = divmod(n, PACK)
             if t == 0:
                 attn_bf[r] = soft.tile([P, PACK, N], BF16, name="attn_bf_t")
-            if n >= SLOTS - 2:
+            if n in VECTOR_NORM:
                 nc.vector.tensor_scalar(
                     out=attn_bf[r][:, t, :], in0=e_sb[n][:], scalar1=r_sum[n][:], scalar2=None, op0=MULT
                 )
@@ -436,9 +439,13 @@ def tile_nonlocalblock_pa_kernel(
             jobs = tensor_jobs.get(n, [])
             run(copy_jobs.get(n, []))
             if 1 <= n:
-                maximum(n - 1)
+                half_maximum(n - 1, 0)
+            if 1 <= n:
+                half_maximum(n - 1, 1)
             if 2 <= n:
                 reciprocal_sum(n - 2)
+            if 1 <= n:
+                maximum(n - 1)
             if 3 <= n:
                 normalise(n - 3)
             if 1 <= n:
@@ -475,13 +482,15 @@ def tile_nonlocalblock_pa_kernel(
             for n in range(SLOTS):
                 slot(n)
             run(copy_jobs.get(SLOTS, []))
+            half_maximum(last, 0)
+            half_maximum(last, 1)
+            reciprocal_sum(last - 1)
             maximum(last)
             normalise(last - 2)
             y_chunks(0, 0, 1)
             exponentials(last)
             run(vector_jobs.get(SLOTS, []))
             y_chunks(0, 1, 4)
-            reciprocal_sum(last - 1)
             normalise(last - 1)
             run(vector_jobs.get(SLOTS + 1, []))
             reciprocal_sum(last)

@@ -13,7 +13,7 @@ MULT = mybir.AluOpType.mult
 MAX = mybir.AluOpType.max
 EXP = mybir.ActivationFunctionType.Exp
 COPY = mybir.ActivationFunctionType.Copy
-IDENT = mybir.ActivationFunctionType.Identity
+POW = mybir.AluOpType.pow
 X_AXIS = mybir.AxisListType.X
 
 B = 2
@@ -41,7 +41,7 @@ W_SLOT = 6
 WQ = 10
 RS = (7, 12, 14)
 E_BUFS = 7
-VECTOR_NORM = (8, 10, 14, 15)
+VECTOR_NORM = (14, 15)
 FLOPS = 3 * 2 * B * N * N * IC
 
 
@@ -66,6 +66,9 @@ def tile_nonlocalblock_pa_kernel(
         make_identity(nc, ident_bf[:])
         ident_f32 = const.tile([P, P], F32, name="ident_f32")
         make_identity(nc, ident_f32[:])
+
+        minus_one = const.tile([P, 1], F32, name="minus_one")
+        nc.gpsimd.memset(minus_one[:], -1.0)
 
         theta_sb = []
         phi_sb = []
@@ -240,13 +243,11 @@ def tile_nonlocalblock_pa_kernel(
                     scale=1.0,
                     accum_out=half_sum[:, ih : ih + 1],
                 )
-            nc.scalar.activation(
-                out=e_sum[n][:], in_=half_sum[:, 0:1], func=IDENT, bias=half_sum[:, 1:2], scale=1.0
-            )
+            nc.gpsimd.tensor_tensor(out=e_sum[n][:], in0=half_sum[:, 0:1], in1=half_sum[:, 1:2], op=ADD)
 
         def reciprocal_sum(n):
             r_sum[n] = stats.tile([P, 1], F32, name="r_sum_t")
-            nc.vector.reciprocal(out=r_sum[n][:], in_=e_sum[n][:])
+            nc.gpsimd.tensor_tensor(out=r_sum[n][:], in0=e_sum[n][:], in1=minus_one[:], op=POW)
 
         def normalise(n):
             r, t = divmod(n, PACK)

from contextlib import ExitStack

import concourse.mybir as mybir
from concourse.masks import make_identity

F32 = mybir.dt.float32
BF16 = mybir.dt.bfloat16
U32 = mybir.dt.uint32
U8 = mybir.dt.uint8
FP8X4 = mybir.dt.float8_e4m3fn_x4
ADD = mybir.AluOpType.add
MULT = mybir.AluOpType.mult
MAX = mybir.AluOpType.max
EXP = mybir.ActivationFunctionType.Exp
COPY = mybir.ActivationFunctionType.Copy
POW = mybir.AluOpType.pow
X_AXIS = mybir.AxisListType.X

B = 2
IC = 512
C = 1024
N = 1024
P = 128
PACK = 4
BANK = 512
K_PASS = P * PACK
J_PASSES = N // K_PASS
J_BLOCKS = N // P
I_HALVES = N // BANK
IC_CHUNKS = IC // P
O_BLOCKS = C // P
I_BLOCKS = N // P
BANK_BLOCKS = BANK // P
SLOTS = B * J_BLOCKS
MATMUL_POS = 5

G_ADD = (3, 7)
G_SLOT = (8, 12)
GQ = (12, 16)
W_SLOT = 6
WQ = 10
RS = (7, 12, 14)
E_BUFS = 7
VECTOR_NORM = (14, 15)
FLOPS = 3 * 2 * B * N * N * IC


def tile_nonlocalblock_pa_kernel(
    tc, theta, phi, g_proj, pos_embedding, pos_embedding_decoder, w_mask, x, out
):
    nc = tc.nc
    x_rows = x.rearrange("b o h w -> b o (h w)")
    out_rows = out.rearrange("b o h w -> b o (h w)")

    with ExitStack() as stack:
        const = stack.enter_context(tc.tile_pool(name="const", bufs=1))
        inputs = stack.enter_context(tc.tile_pool(name="inputs", bufs=2))
        soft = stack.enter_context(tc.tile_pool(name="soft", bufs=2))
        stats = stack.enter_context(tc.tile_pool(name="stats", bufs=8))
        codes = stack.enter_context(tc.tile_pool(name="codes", bufs=2))
        late = stack.enter_context(tc.tile_pool(name="late", bufs=1))
        psum_acc = stack.enter_context(tc.psum_pool(name="psum_acc", bufs=6))
        psum_tp = stack.enter_context(tc.psum_pool(name="psum_tp", bufs=2))

        ident_bf = const.tile([P, P], BF16, name="ident_bf")
        make_identity(nc, ident_bf[:])
        ident_f32 = const.tile([P, P], F32, name="ident_f32")
        make_identity(nc, ident_f32[:])

        minus_one = const.tile([P, 1], F32, name="minus_one")
        nc.gpsimd.memset(minus_one[:], -1.0)

        theta_sb = []
        phi_sb = []
        gp_sb = []
        for b in range(B):
            theta_sb.append([inputs.tile([P, IC_CHUNKS, BANK], BF16, name="theta_sb", tag="theta%d" % h) for h in range(2)])
            phi_sb.append([inputs.tile([P, IC_CHUNKS, K_PASS], BF16, name="phi_sb", tag="phi%d" % h) for h in range(2)])
            gp_sb.append(inputs.tile([P, PACK, N], BF16, name="gp_sb", tag="gp"))
        pos_sb = []
        for g in range(J_PASSES):
            pos_sb.append(
                [late.tile([P, BANK_BLOCKS, K_PASS], BF16, name="pos_sb", tag="pos%d" % (2 * g + ih)) for ih in range(2)]
            )
        ped_sb = const.tile([P, PACK, N], BF16, name="ped_sb")
        w_sb = late.tile([P, O_BLOCKS, IC], BF16, name="w_sb", tag="y_grouped", align_bytes=64)

        def load_theta(b, ih):
            cols = slice(ih * BANK, (ih + 1) * BANK)
            nc.sync.dma_start(
                out=theta_sb[b][ih][:], in_=theta[b, :, cols].rearrange("(k p) i -> p k i", p=P)
            )

        def load_phi(b, g):
            cols = slice(g * K_PASS, (g + 1) * K_PASS)
            nc.sync.dma_start(
                out=phi_sb[b][g][:], in_=phi[b, :, cols].rearrange("(k p) j -> p k j", p=P)
            )

        def load_pos(g, ih):
            cols = slice(g * K_PASS, (g + 1) * K_PASS)
            rows = slice(ih * BANK, (ih + 1) * BANK)
            nc.sync.dma_start(
                out=pos_sb[g][ih][:],
                in_=pos_embedding[0, rows, cols].rearrange("(a p) j -> p a j", p=P),
            )

        def load_rows(tile, rows, u):
            nc.sync.dma_start(
                out=tile[:, 2 * u : 2 * u + 2, :].rearrange("p e j -> p (e j)"),
                in_=rows[u * 2 * P : (u + 1) * 2 * P, :].rearrange("(p e) j -> p (e j)", p=P),
            )

        def load_x(b):
            quarters = []
            for q in range(4):
                if b == 0:
                    x_q = late.tile([P, O_BLOCKS // 4, N], BF16, name="x_q", tag="x%d" % q)
                else:
                    x_q = inputs.tile([P, O_BLOCKS // 4, N], BF16, name="x_q", tag=("theta0", "theta1", "phi0", "phi1")[q])
                rows = slice(q * (C // 4), (q + 1) * (C // 4))
                nc.sync.dma_start(out=x_q[:], in_=x_rows[b, rows, :].rearrange("(a p) i -> p a i", p=P))
                quarters.append(x_q)
            return quarters

        for k in range(0, IC_CHUNKS, 2):
            ks = slice(k, k + 2)
            rows = slice(k * P, (k + 2) * P)
            nc.sync.dma_start(
                out=theta_sb[0][0][:, ks, :], in_=theta[0, rows, 0:BANK].rearrange("(k p) i -> p k i", p=P)
            )
            nc.sync.dma_start(
                out=phi_sb[0][0][:, ks, :], in_=phi[0, rows, 0:K_PASS].rearrange("(k p) j -> p k j", p=P)
            )
        load_pos(0, 0)
        load_theta(0, 1)
        load_pos(0, 1)
        load_phi(0, 1)
        load_pos(1, 0)
        load_pos(1, 1)
        for u in range(2):
            load_rows(ped_sb, pos_embedding_decoder[0].rearrange("c h w -> c (h w)"), u)
            load_rows(gp_sb[0], g_proj[0], u)
        nc.sync.dma_start(out=w_sb[:], in_=w_mask.rearrange("(a p) c -> p a c", p=P))
        load_theta(1, 0)
        load_phi(1, 0)
        load_theta(1, 1)
        for u in range(2):
            load_rows(gp_sb[1], g_proj[1], u)
        load_phi(1, 1)

        first_col = (MATMUL_POS - PACK) * P
        pos32 = []
        for ih in range(I_HALVES):
            pos32.append(const.tile([P, BANK_BLOCKS, K_PASS - first_col], F32, name="pos32_t", tag="pos32_%d" % ih))
            nc.gpsimd.tensor_scalar(
                out=pos32[ih][:], in0=pos_sb[1][ih][:, :, first_col:], scalar1=1.0, scalar2=0.0, op0=MULT, op1=ADD
            )
        tp_tiles = {}

        x_sb = [load_x(0)]

        acc = {}
        e_sum = {}
        neg_max = {}
        half_max = {}
        o_sb = {}
        r_sum = {}
        e_sb = {}
        attn_bf = {}
        grouped = {}
        attn_codes = []
        attn_scales = []
        g_grouped = {}
        g_bf = {}
        g_codes = []
        g_scales = []
        for b in range(B):
            attn_codes.append(codes.tile([P, J_PASSES, N], U32, name="attn_codes", align_bytes=64))
            attn_scales.append(codes.tile([P, J_PASSES, N], U8, name="attn_scales", align_bytes=64))
            g_codes.append(codes.tile([P, J_PASSES, IC], U32, name="g_codes", align_bytes=64))
            g_scales.append(codes.tile([P, J_PASSES, IC], U8, name="g_scales", align_bytes=64))
        w_grouped = const.tile([P, C * PACK], BF16, name="w_grouped", align_bytes=64)
        w_codes = const.tile([P, C], U32, name="w_codes", align_bytes=64)
        w_scales = const.tile([P, C], U8, name="w_scales", align_bytes=64)
        y_grouped = {}
        y_codes = {}
        y_scales = {}

        def scores(n, ih):
            b, jb = divmod(n, J_BLOCKS)
            g, t = divmod(jb, PACK)
            m = n * I_HALVES + ih
            acc[m] = psum_acc.tile([P, BANK], F32, name="acc")
            for k in range(IC_CHUNKS):
                nc.tensor.matmul(
                    out=acc[m][:],
                    lhsT=phi_sb[b][g][:, k, t * P : (t + 1) * P],
                    rhs=theta_sb[b][ih][:, k, :],
                    start=(k == 0),
                    stop=False,
                )
            for a in range(BANK_BLOCKS):
                if jb < MATMUL_POS:
                    nc.tensor.matmul(
                        out=acc[m][:, a * P : (a + 1) * P],
                        lhsT=pos_sb[g][ih][:, a, t * P : (t + 1) * P],
                        rhs=ident_bf[:],
                        start=False,
                        stop=(a == BANK_BLOCKS - 1),
                    )
                else:
                    nc.tensor.matmul(
                        out=acc[m][:, a * P : (a + 1) * P],
                        lhsT=pos32[ih][:, a, t * P - first_col : (t + 1) * P - first_col],
                        rhs=ident_f32[:],
                        is_transpose=True,
                        start=False,
                        stop=(a == BANK_BLOCKS - 1),
                    )

        def half_maximum(n, ih):
            if ih == 0:
                half_max[n] = stats.tile([P, I_HALVES], F32, name="half_max_t")
            nc.vector.tensor_reduce(
                out=half_max[n][:, ih : ih + 1], in_=acc[n * I_HALVES + ih][:], axis=X_AXIS, op=MAX
            )

        def maximum(n):
            neg_max[n] = stats.tile([P, 1], F32, name="neg_max_t")
            nc.vector.tensor_reduce(out=neg_max[n][:], in_=half_max[n][:], axis=X_AXIS, op=MAX, negate=True)

        def exponentials(n):
            e_sb[n] = soft.tile([P, N], F32, name="e_sb_t", bufs=E_BUFS)
            e_sum[n] = stats.tile([P, 1], F32, name="e_sum_t")
            half_sum = stats.tile([P, I_HALVES], F32, name="half_sum")
            for ih in range(I_HALVES):
                nc.scalar.activation(
                    out=e_sb[n][:, ih * BANK : (ih + 1) * BANK],
                    in_=acc[n * I_HALVES + ih][:],
                    func=EXP,
                    bias=neg_max[n][:],
                    scale=1.0,
                    accum_out=half_sum[:, ih : ih + 1],
                )
            nc.gpsimd.tensor_tensor(out=e_sum[n][:], in0=half_sum[:, 0:1], in1=half_sum[:, 1:2], op=ADD)

        def reciprocal_sum(n):
            r_sum[n] = stats.tile([P, 1], F32, name="r_sum_t")
            nc.gpsimd.tensor_tensor(out=r_sum[n][:], in0=e_sum[n][:], in1=minus_one[:], op=POW)

        def normalise(n):
            r, t = divmod(n, PACK)
            if t == 0:
                attn_bf[r] = soft.tile([P, PACK, N], BF16, name="attn_bf_t")
            if n in VECTOR_NORM:
                nc.vector.tensor_scalar(
                    out=attn_bf[r][:, t, :], in0=e_sb[n][:], scalar1=r_sum[n][:], scalar2=None, op0=MULT
                )
            else:
                nc.scalar.activation(out=attn_bf[r][:, t, :], in_=e_sb[n][:], func=COPY, scale=r_sum[n][:])

        def regroup(r, first, last, engine_copy):
            if first == 0:
                grouped[r] = soft.tile([P, N, PACK], BF16, name="grouped_t", align_bytes=64)
            cols = slice(first, last)
            engine_copy(
                out=grouped[r][:, cols, :].rearrange("p (c i) t -> p c t i", i=4),
                in_=attn_bf[r][:, :, cols].rearrange("p t (c i) -> p c t i", i=4),
            )

        def quantise_attn(r, first, last):
            b, g = divmod(r, J_PASSES)
            cols = slice(first, last)
            nc.vector.quantize_mx(
                out=attn_codes[b][:, g, cols].bitcast(FP8X4),
                scales=attn_scales[b][:, g, cols],
                in_=grouped[r][:, cols, :].rearrange("p i t -> p (i t)"),
            )

        def g_add(b, row):
            if row == 0:
                if b == 0:
                    g_bf[b] = soft.tile([P, PACK, N], BF16, name="g_bf_t", bufs=1)
                else:
                    g_bf[b] = inputs.tile([P, PACK, N], BF16, name="g_bf_t", tag="gp")
            pairs = "p (u e w) -> p u w e"
            nc.vector.tensor_tensor(
                out=g_bf[b][:, row, :].rearrange("p (u w e) -> p u w e", w=P, e=2),
                in0=gp_sb[b][:, row, :].rearrange(pairs, e=2, w=P),
                in1=ped_sb[:, row, :].rearrange(pairs, e=2, w=P),
                op=ADD,
            )

        def g_tile(b, k):
            half, g = divmod(k, J_PASSES)
            if k == 0:
                g_grouped[b] = soft.tile([P, J_PASSES, IC, PACK], BF16, name="g_grouped_t", bufs=1, align_bytes=64)
            pg = psum_tp.tile([P, 2, 2, P], F32, name="pg", tag="tp")
            tp_tiles["g", b, k] = pg
            for a in range(2):
                words = g_bf[b][:, 2 * half + a, :].bitcast(F32)
                for u in range(2):
                    first = (2 * g + u) * P
                    nc.tensor.transpose(pg[:, a, u, :], words[:, first : first + P], ident_f32[:])

        def g_tile_out(b, k):
            half, g = divmod(k, J_PASSES)
            words = g_grouped[b][:].rearrange("p g c t -> p (g c t)").bitcast(F32).rearrange("p (g c u) -> p g c u", g=2, u=2)
            nc.scalar.copy(
                out=words[:, g, 2 * half * P : (2 * half + 2) * P, :].rearrange("p (a c) u -> p a c u", a=2),
                in_=tp_tiles["g", b, k][:].rearrange("p a u c -> p a c u"),
            )

        def g_quantise(b):
            nc.vector.quantize_mx(
                out=g_codes[b][:].rearrange("p g c -> p (g c)").bitcast(FP8X4),
                scales=g_scales[b][:].rearrange("p g c -> p (g c)"),
                in_=g_grouped[b][:].rearrange("p g c t -> p (g c t)"),
            )

        def w_tile(k):
            pw = psum_tp.tile([P, 2, 2 * P], F32, name="pw", tag="tp")
            tp_tiles["w", k] = pw
            for u in range(2):
                for a in range(2):
                    nc.tensor.transpose(
                        pw[:, u, a * P : (a + 1) * P],
                        w_sb[:, 2 * k + a, :].bitcast(F32)[:, u * P : (u + 1) * P],
                        ident_f32[:],
                    )

        def w_tile_out(k):
            words = w_grouped[:].bitcast(F32).rearrange("p (o u) -> p o u", u=2)
            nc.scalar.copy(
                out=words[:, 2 * k * P : (2 * k + 2) * P, :], in_=tp_tiles["w", k][:].rearrange("p u o -> p o u")
            )

        def w_quantise():
            nc.vector.quantize_mx(out=w_codes[:].bitcast(FP8X4), scales=w_scales[:], in_=w_grouped[:])

        def y_chunk(b, ic):
            if ic == 0:
                y_grouped[b] = late.tile([P, N, PACK], BF16, name="y_grouped", align_bytes=64)
            i_cols = slice(ic * P, (ic + 1) * P)
            if ic % 2 == 0:
                yt = psum_tp.tile([P, PACK, P], F32, name="yt", tag="tp")
            else:
                yt = psum_acc.tile([P, PACK, P], F32, name="yt", tag="acc")
            tp_tiles["y", b, ic] = yt
            for t in range(PACK):
                c_cols = slice(t * P, (t + 1) * P)
                for g in range(J_PASSES):
                    nc.tensor.matmul_mx(
                        out=yt[:, t, :],
                        lhsT=g_codes[b][:, g, c_cols].bitcast(FP8X4),
                        lhsT_scale=g_scales[b][:, g, c_cols],
                        rhs=attn_codes[b][:, g, i_cols].bitcast(FP8X4),
                        rhs_scale=attn_scales[b][:, g, i_cols],
                        start=(g == 0),
                        stop=(g == J_PASSES - 1),
                    )

        def y_chunk_out(b, ic):
            dst = y_grouped[b][:, ic * P : (ic + 1) * P, :]
            src = tp_tiles["y", b, ic][:].rearrange("p t i -> p i t")
            nc.scalar.copy(out=dst, in_=src)

        def y_quantise(b, ih):
            if ih == 0:
                y_codes[b] = late.tile([P, N], U32, name="y_codes", bufs=2, align_bytes=64)
                y_scales[b] = late.tile([P, N], U8, name="y_scales", bufs=2, align_bytes=64)
            cols = slice(ih * BANK, (ih + 1) * BANK)
            nc.vector.quantize_mx(
                out=y_codes[b][:, cols].bitcast(FP8X4),
                scales=y_scales[b][:, cols],
                in_=y_grouped[b][:, cols, :].rearrange("p i t -> p (i t)"),
            )

        def m_tile(b, ih, ob):
            cols = slice(ih * BANK, (ih + 1) * BANK)
            o_cols = slice(ob * P, (ob + 1) * P)
            m_acc = psum_acc.tile([P, BANK], F32, name="m_acc", tag="acc")
            tp_tiles["m", b, ih, ob] = m_acc
            nc.tensor.matmul_mx(
                out=m_acc[:],
                lhsT=w_codes[:, o_cols].bitcast(FP8X4),
                lhsT_scale=w_scales[:, o_cols],
                rhs=y_codes[b][:, cols].bitcast(FP8X4),
                rhs_scale=y_scales[b][:, cols],
                start=True,
                stop=True,
            )

        def m_pair(b, ih, pair):
            cols = slice(ih * BANK, (ih + 1) * BANK)
            o_tile = soft.tile([P, 2, BANK], F32, name="o_tile", tag="e_sb_t", bufs=E_BUFS)
            o_sb[b, ih, pair] = o_tile
            for a in range(2):
                m_tile(b, ih, 2 * pair + a)
                m_acc = tp_tiles["m", b, ih, 2 * pair + a]
                x_cols = x_sb[b][pair][:, a, cols]
                nc.vector.tensor_tensor(out=o_tile[:, a, :], in0=m_acc[:], in1=x_cols, op=ADD)

        def m_store(b, ih, pair):
            cols = slice(ih * BANK, (ih + 1) * BANK)
            rows = slice(2 * pair * P, (2 * pair + 2) * P)
            nc.sync.dma_start(
                out=out_rows[b, rows, cols].rearrange("(a p) i -> p a i", p=P), in_=o_sb[b, ih, pair][:]
            )

        tensor_jobs = {}
        copy_jobs = {}
        vector_jobs = {}

        def put(table, slot, job, *args):
            table.setdefault(slot, []).append((job, args))

        def run(jobs):
            for job, args in jobs:
                job(*args)

        for b in range(B):
            for row in range(PACK):
                put(vector_jobs, G_ADD[b] + row, g_add, b, row)
            for k in range(PACK):
                put(tensor_jobs, G_SLOT[b] + k // 2, g_tile, b, k)
                put(copy_jobs, G_SLOT[b] + k // 2 + 1, g_tile_out, b, k)
            put(vector_jobs, GQ[b], g_quantise, b)
        for k in range(O_BLOCKS // 2):
            put(tensor_jobs, W_SLOT + k // 2, w_tile, k)
            put(copy_jobs, W_SLOT + k // 2 + 1, w_tile_out, k)
        put(vector_jobs, WQ, w_quantise)
        for r in range(B * J_PASSES - 1):
            for ih in range(I_HALVES):
                put(vector_jobs, RS[r] + ih, regroup, r, ih * BANK, (ih + 1) * BANK, nc.vector.tensor_copy)
            put(vector_jobs, RS[r] + 2, quantise_attn, r, 0, N)

        def slot(n):
            jobs = tensor_jobs.get(n, [])
            run(copy_jobs.get(n, []))
            if 1 <= n:
                half_maximum(n - 1, 0)
            if 1 <= n:
                half_maximum(n - 1, 1)
            if 2 <= n:
                reciprocal_sum(n - 2)
            if 1 <= n:
                maximum(n - 1)
            if 3 <= n:
                normalise(n - 3)
            if 1 <= n:
                exponentials(n - 1)
            if n == 0:
                scores(0, 0)
                scores(1, 0)
                scores(0, 1)
            elif n == 1:
                scores(1, 1)
            else:
                scores(n, 0)
                run(jobs[: len(jobs) // 2])
                scores(n, 1)
                run(jobs[len(jobs) // 2 :])
            run(vector_jobs.get(n, []))
            if n == 8:
                x_sb.append(load_x(1))

        last = SLOTS - 1
        r = B * J_PASSES - 1

        def y_chunks(b, first, end):
            for ic in range(first, end):
                y_chunk(b, ic)
                y_chunk_out(b, ic)

        def m_row(b, ih, pairs):
            for pair in pairs:
                m_pair(b, ih, pair)
                m_store(b, ih, pair)

        with tc.manual_schedule():
            for n in range(SLOTS):
                slot(n)
            run(copy_jobs.get(SLOTS, []))
            half_maximum(last, 0)
            half_maximum(last, 1)
            reciprocal_sum(last - 1)
            maximum(last)
            normalise(last - 2)
            y_chunks(0, 0, 1)
            exponentials(last)
            run(vector_jobs.get(SLOTS, []))
            y_chunks(0, 1, 4)
            normalise(last - 1)
            run(vector_jobs.get(SLOTS + 1, []))
            reciprocal_sum(last)
            normalise(last)
            y_quantise(0, 0)
            regroup(r, 0, BANK, nc.vector.tensor_copy)
            y_chunks(0, 4, 8)
            regroup(r, BANK, N, nc.scalar.copy)
            m_row(0, 0, (0,))
            quantise_attn(r, 0, BANK)
            y_quantise(0, 1)
            m_row(0, 0, (1,))
            quantise_attn(r, BANK, N)
            y_chunks(1, 0, 2)
            m_row(0, 0, (2,))
            y_chunks(1, 2, 4)
            m_row(0, 0, (3,))
            m_row(0, 1, (0,))
            y_quantise(1, 0)
            y_chunks(1, 4, 6)
            m_row(0, 1, (1,))
            y_chunks(1, 6, 8)
            m_row(0, 1, (2,3))
            y_quantise(1, 1)
            m_row(1, 0, range(4))
            m_row(1, 1, range(4))
